import numpy as np
import ml_dtypes


def mxq(x, axis, fmt="e4m3"):
    dtype, down = {"e4m3": (ml_dtypes.float8_e4m3fn, 7), "e5m2": (ml_dtypes.float8_e5m2, 14)}[fmt]
    v = np.moveaxis(np.asarray(x, np.float32).astype(ml_dtypes.bfloat16).astype(np.float64), axis, -1)
    blocks = v.reshape(v.shape[:-1] + (-1, 32))
    amax = np.abs(blocks).max(-1, keepdims=True)
    byte = np.maximum(np.where(amax > 0, np.frexp(amax)[1] - 1 + 127, 0) - down, 1)
    scale = np.exp2(byte - 127.0)
    codes = (blocks / scale).astype(np.float32).astype(dtype).astype(np.float64)
    return np.moveaxis((codes * scale).reshape(v.shape), -1, axis)


WIDE = False


def mx_kscale(k):
    if not WIDE:
        return np.ones(k)
    levels = np.array([10, -10, 5, -5, 0])
    a = np.random.permutation(np.resize(levels, k // 512 * 4)).reshape(k // 512, 4)
    idx = np.arange(k)
    return np.exp2(a[idx // 512, idx % 128 // 32])


BF16 = ml_dtypes.bfloat16


def bf(x):
    return np.asarray(x, np.float32).astype(BF16)


def f64(x):
    return np.asarray(x).astype(np.float64)


B, C, P, PB, D, H = 1, 1024, 4, 1, 1024, 2
R = D // H


def setup_inputs():
    t = np.tile(mx_kscale(R), H)[None, :, None]
    ws = 1.5 / np.sqrt(D)
    return {"qz": bf(np.random.standard_normal((B, C, PB, D))),
            "channel_u_w": bf(np.random.standard_normal((B, D, D)) * ws * t),
            "channel_v_w": bf(np.random.standard_normal((B, D, D)) * ws / t)}


def reference(qz, channel_u_w, channel_v_w):
    x = f64(qz)
    xq = mxq(x, 3, "e4m3").reshape(B, C * PB, D)
    qu = xq @ mxq(f64(channel_u_w), 2, "e4m3").transpose(0, 2, 1)
    qv = xq @ mxq(f64(channel_v_w), 2, "e4m3").transpose(0, 2, 1)
    qu = qu.reshape(B, C, PB, H, R).transpose(0, 2, 3, 1, 4)
    qv = qv.reshape(B, C, PB, H, R).transpose(0, 2, 3, 1, 4)
    logits = (mxq(qu, 4, "e4m3") @ mxq(qv, 4, "e4m3").transpose(0, 1, 2, 4, 3)) * (1.0 / np.sqrt(R))
    e = np.exp(logits - logits.max(-1, keepdims=True))
    attn = e / e.sum(-1, keepdims=True)
    m = (attn * x.transpose(0, 2, 1, 3)[:, :, None, :, :]).mean(axis=2)
    return m.transpose(0, 2, 1, 3)

@@ -1,0 +1,289 @@
+import math
+from contextlib import ExitStack
+
+import concourse.mybir as mybir
+from concourse.masks import make_identity
+
+F32 = mybir.dt.float32
+BF16 = mybir.dt.bfloat16
+U32 = mybir.dt.uint32
+U8 = mybir.dt.uint8
+FP8X4 = mybir.dt.float8_e4m3fn_x4
+ALU = mybir.AluOpType
+EXP = mybir.ActivationFunctionType.Exp
+
+P = 128
+PACK = 4
+K_PASS = P * PACK
+C = 1024
+D = 1024
+HEADS = 2
+R = D // HEADS
+C_TILES = C // P
+D_PASSES = D // K_PASS
+BANK = 512
+E_BANKS = C // BANK
+
+FLOPS = 2 * C * D * (2 * D) + HEADS * 2 * C * C * R
+
+
+def tile_dynamicptheadselection_pa_kernel(tc, qz, channel_u_w, channel_v_w, out):
+    nc = tc.nc
+
+    x_dram = qz.flatten_outer_dims().rearrange("(j p) d -> p j d", p=P)
+    out_dram = out.flatten_outer_dims().rearrange("(j p) e -> p j e", p=P)
+    w_dram = {
+        "u": channel_u_w.flatten_outer_dims().rearrange("(h p t) d -> h p t d", h=HEADS, t=PACK),
+        "v": channel_v_w.flatten_outer_dims().rearrange("(h p t) d -> h p t d", h=HEADS, t=PACK),
+    }
+
+    with ExitStack() as ctx:
+        ctx.enter_context(tc.manual_schedule())
+        keep = ctx.enter_context(tc.tile_pool(name="keep", bufs=1))
+        staging = ctx.enter_context(tc.tile_pool(name="staging", bufs=2))
+        results = ctx.enter_context(tc.tile_pool(name="results", bufs=4))
+        banks = ctx.enter_context(tc.psum_pool(name="banks", bufs=8))
+
+        x_rows = keep.tile([P, C_TILES, D], BF16, name="x_rows")
+        w_rows = {}
+        for h in range(HEADS):
+            for w in ("v", "u"):
+                w_rows[w, h] = keep.tile([P, PACK, D], BF16, name="%s%d_rows" % (w, h))
+
+        def load_weights(w, h):
+            for t in range(0, PACK, 2):
+                nc.sync.dma_start(out=w_rows[w, h][:, t : t + 2, :], in_=w_dram[w][h, :, t : t + 2, :])
+
+        load_weights("v", 0)
+        for j in range(0, C_TILES, 2):
+            nc.sync.dma_start(out=x_rows[:, j : j + 2, :], in_=x_dram[:, j : j + 2, :])
+        load_weights("u", 0)
+        load_weights("v", 1)
+        load_weights("u", 1)
+
+        identity = keep.tile([P, P], F32, name="identity")
+        make_identity(nc, identity[:])
+        table_warmer = keep.tile([P, 1], F32, name="table_warmer")
+        nc.scalar.activation(out=table_warmer[:], in_=identity[:, 0:1], func=EXP)
+
+        def copy_out(out_view, bank_view, on_vector):
+            if on_vector:
+                nc.vector.tensor_copy(out=out_view, in_=bank_view)
+            else:
+                nc.scalar.copy(out=out_view, in_=bank_view)
+
+        def quantise(grouped, codes, scales):
+            nc.vector.quantize_mx(out=codes.bitcast(FP8X4), scales=scales, in_=grouped)
+
+        def transpose_row_tile(rows, grouped, first_column, on_vector):
+            words = rows.bitcast(F32)
+            bank = banks.tile([P, 2 * D_PASSES, P], F32, tag="bank", name="transposed")
+            for k in range(2 * D_PASSES):
+                nc.tensor.transpose(bank[:, k, :], words[:, k * P : (k + 1) * P], identity[:])
+            grouped_words = grouped.bitcast(F32).rearrange("p g (c u) -> p g c u", u=2)
+            copy_out(
+                grouped_words[:, :, first_column : first_column + P, :],
+                bank[:].rearrange("p (g u) c -> p g c u", u=2),
+                on_vector,
+            )
+
+        x_grouped = keep.tile([P, D_PASSES, C * PACK], BF16, name="x_grouped", align_bytes=64)
+        x_codes = keep.tile([P, D_PASSES, C], U32, name="x_codes", align_bytes=64)
+        x_scales = keep.tile([P, D_PASSES, C], U8, name="x_scales", align_bytes=64)
+        w_grouped = {}
+        w_codes = {}
+        w_scales = {}
+        q_grouped = {}
+        q_codes = {}
+        q_scales = {}
+
+        def quantise_x_pair(pair):
+            channels = slice(2 * pair * P, 2 * (pair + 1) * P)
+            values = slice(2 * pair * P * PACK, 2 * (pair + 1) * P * PACK)
+            for g in range(D_PASSES):
+                quantise(x_grouped[:, g, values], x_codes[:, g, channels], x_scales[:, g, channels])
+
+        def transpose_weights(w, h, share_with_vector):
+            w_grouped[w, h] = staging.tile(
+                [P, D_PASSES, R * PACK], BF16, tag="w_grouped", name="w_grouped", align_bytes=64
+            )
+            for t in range(PACK):
+                transpose_row_tile(w_rows[w, h][:, t, :], w_grouped[w, h][:], t * P, share_with_vector and t % 2 == 1)
+
+        def quantise_weights(w, h):
+            w_codes[w, h] = keep.tile([P, D_PASSES, R], U32, name="%s%d_codes" % (w, h), align_bytes=64)
+            w_scales[w, h] = keep.tile([P, D_PASSES, R], U8, name="%s%d_scales" % (w, h), align_bytes=64)
+            for g in range(D_PASSES):
+                quantise(w_grouped[w, h][:, g, :], w_codes[w, h][:, g, :], w_scales[w, h][:, g, :])
+            q_grouped[w, h] = keep.tile([P, C, PACK], BF16, name="q%s%d_grouped" % (w, h), align_bytes=64)
+            q_codes[w, h] = keep.tile([P, C], U32, name="q%s%d_codes" % (w, h), align_bytes=64)
+            q_scales[w, h] = keep.tile([P, C], U8, name="q%s%d_scales" % (w, h), align_bytes=64)
+
+        def project(w, h, j, on_vector):
+            channels = slice(j * P, (j + 1) * P)
+            bank = banks.tile([P, PACK, P], F32, tag="bank", name="projected")
+            for t in range(PACK):
+                rows_t = slice(t * P, (t + 1) * P)
+                for g in range(D_PASSES):
+                    nc.tensor.matmul_mx(
+                        out=bank[:, t, :],
+                        lhsT=w_codes[w, h][:, g, rows_t].bitcast(FP8X4),
+                        lhsT_scale=w_scales[w, h][:, g, rows_t],
+                        rhs=x_codes[:, g, channels].bitcast(FP8X4),
+                        rhs_scale=x_scales[:, g, channels],
+                        start=(g == 0),
+                        stop=(g == D_PASSES - 1),
+                    )
+            copy_out(q_grouped[w, h][:, channels, :], bank[:].rearrange("p t c -> p c t"), on_vector)
+
+        def quantise_projection(w, h, first, count):
+            channels = slice(first, first + count)
+            quantise(
+                q_grouped[w, h][:, channels, :].rearrange("p c t -> p (c t)"),
+                q_codes[w, h][:, channels],
+                q_scales[w, h][:, channels],
+            )
+
+        lowest = keep.tile([P, HEADS, C_TILES, E_BANKS], F32, name="lowest")
+        sums = keep.tile([P, C_TILES, HEADS], F32, name="sums")
+
+        def logit_banks(h, j):
+            queries = slice(j * P, (j + 1) * P)
+            filled = []
+            for i in range(E_BANKS):
+                keys = slice(i * BANK, (i + 1) * BANK)
+                bank = banks.tile([P, BANK], F32, tag="bank", name="logit_bank")
+                nc.tensor.matmul_mx(
+                    out=bank[:],
+                    lhsT=q_codes["u", h][:, queries].bitcast(FP8X4),
+                    lhsT_scale=q_scales["u", h][:, queries],
+                    rhs=q_codes["v", h][:, keys].bitcast(FP8X4),
+                    rhs_scale=q_scales["v", h][:, keys],
+                    start=True,
+                    stop=True,
+                )
+                filled.append(bank)
+            return filled
+
+        def fold_bank(h, j, i, bank, negated):
+            nc.vector.tensor_scalar(
+                out=negated[:, i * BANK : (i + 1) * BANK],
+                in0=bank[:],
+                scalar1=-1.0 / math.sqrt(R),
+                scalar2=(None if i == 0 else lowest[:, h, j, i - 1 : i]),
+                op0=ALU.mult,
+                op1=ALU.min,
+                accum_out=lowest[:, h, j, i : i + 1],
+            )
+
+        def exponentials(h, j, negated):
+            nc.scalar.activation(
+                out=negated,
+                in_=negated,
+                func=EXP,
+                bias=lowest[:, h, j, E_BANKS - 1 : E_BANKS],
+                scale=-1.0,
+                accum_out=sums[:, j, h : h + 1],
+            )
+
+        inverse = keep.tile([P, C_TILES, HEADS], F32, name="inverse")
+        ratio = keep.tile([P, C_TILES], F32, name="ratio")
+        half_inverse = keep.tile([P, C_TILES], F32, name="half_inverse")
+
+        def invert_sums(j):
+            nc.vector.reciprocal(out=inverse[:, j, :], in_=sums[:, j, :])
+
+        def coefficients(j):
+            nc.vector.tensor_tensor(out=ratio[:, j : j + 1], in0=sums[:, j, 1:2], in1=inverse[:, j, 0:1], op=ALU.mult)
+            nc.vector.tensor_scalar(
+                out=half_inverse[:, j : j + 1], in0=inverse[:, j, 1:2], scalar1=0.5, scalar2=None, op0=ALU.mult
+            )
+
+        def mix_heads(j, exp0, exp1):
+            nc.vector.scalar_tensor_tensor(
+                out=exp1, in0=exp0, scalar=ratio[:, j : j + 1], in1=exp1, op0=ALU.mult, op1=ALU.add
+            )
+
+        def scale_and_store(j, mixed):
+            nc.vector.scalar_tensor_tensor(
+                out=mixed, in0=mixed, scalar=half_inverse[:, j : j + 1], in1=x_rows[:, j, :], op0=ALU.mult, op1=ALU.mult
+            )
+            nc.sync.dma_start(out=out_dram[:, j, :], in_=mixed)
+
+        transpose_weights("v", 0, True)
+        for pair in range(C_TILES // 2):
+            transpose_row_tile(x_rows[:, 2 * pair, :], x_grouped[:], 2 * pair * P, False)
+            transpose_row_tile(x_rows[:, 2 * pair + 1, :], x_grouped[:], (2 * pair + 1) * P, True)
+            if pair == 0:
+                quantise_weights("v", 0)
+            else:
+                quantise_x_pair(pair - 1)
+        project("v", 0, 0, False)
+        project("v", 0, 1, True)
+        quantise_x_pair(C_TILES // 2 - 1)
+        project("v", 0, 2, False)
+        project("v", 0, 3, True)
+        transpose_weights("u", 0, True)
+        quantise_projection("v", 0, 0, BANK)
+        project("v", 0, 4, False)
+        project("v", 0, 5, True)
+        quantise_weights("u", 0)
+        project("v", 0, 6, False)
+        project("v", 0, 7, True)
+
+        def project_queries(n):
+            if n < HEADS * C_TILES:
+                project("u", n // C_TILES, n % C_TILES, False)
+
+        def quantise_queries(n):
+            if n < HEADS * C_TILES:
+                quantise_projection("u", n // C_TILES, (n % C_TILES) * P, P)
+
+        def project_keys(h, i):
+            for j in range(i * PACK, (i + 1) * PACK):
+                project("v", h, j, False)
+
+        project_queries(0)
+        quantise_projection("v", 0, BANK, BANK)
+        project_queries(1)
+        quantise_queries(0)
+
+        stages = (
+            (lambda: transpose_weights("v", 1, False), lambda: quantise_weights("v", 1)),
+            (lambda: transpose_weights("u", 1, False), lambda: quantise_weights("u", 1)),
+            (lambda: project_keys(1, 0), lambda: quantise_projection("v", 1, 0, BANK)),
+            (lambda: project_keys(1, 1), lambda: quantise_projection("v", 1, BANK, BANK)),
+        )
+        exp_head0 = keep.tile([P, C_TILES, C], F32, name="exp_head0")
+        for j in range(C_TILES):
+            four_banks, then_quantise = stages[j // 2]
+            filled = logit_banks(0, j)
+            project_queries(j + 2)
+            if j % 2 == 0:
+                four_banks()
+            fold_bank(0, j, 0, filled[0], exp_head0[:, j, :])
+            quantise_queries(j + 1)
+            if j % 2 == 1:
+                then_quantise()
+            fold_bank(0, j, 1, filled[1], exp_head0[:, j, :])
+
+        exp_head1 = {}
+        for j in range(C_TILES + 1):
+            if j < C_TILES:
+                exp_head1[j] = results.tile([P, C], F32, tag="exp_head1", name="exp_head1")
+                filled = logit_banks(1, j)
+                project_queries(C_TILES + j + 2)
+                exponentials(0, j, exp_head0[:, j, :])
+                fold_bank(1, j, 0, filled[0], exp_head1[j][:])
+            if j > 0:
+                invert_sums(j - 1)
+            if j < C_TILES:
+                quantise_queries(C_TILES + j + 1)
+            if j > 0:
+                coefficients(j - 1)
+                mix_heads(j - 1, exp_head0[:, j - 1, :], exp_head1[j - 1][:])
+            if j < C_TILES:
+                fold_bank(1, j, 1, filled[1], exp_head1[j][:])
+                exponentials(1, j, exp_head1[j][:])
+            if j > 0:
+                scale_and_store(j - 1, exp_head1[j - 1][:])

@@ -23,6 +23,7 @@ C_TILES = C // P
 D_PASSES = D // K_PASS
 BANK = 512
 E_BANKS = C // BANK
+LAG = 2
 
 FLOPS = 2 * C * D * (2 * D) + HEADS * 2 * C * C * R
 
@@ -41,7 +42,7 @@ def tile_dynamicptheadselection_pa_kernel(tc, qz, channel_u_w, channel_v_w, out)
         ctx.enter_context(tc.manual_schedule())
         keep = ctx.enter_context(tc.tile_pool(name="keep", bufs=1))
         staging = ctx.enter_context(tc.tile_pool(name="staging", bufs=2))
-        results = ctx.enter_context(tc.tile_pool(name="results", bufs=4))
+        results = ctx.enter_context(tc.tile_pool(name="results", bufs=LAG + 3))
         banks = ctx.enter_context(tc.psum_pool(name="banks", bufs=8))
 
         x_rows = keep.tile([P, C_TILES, D], BF16, name="x_rows")
@@ -145,7 +146,8 @@ def tile_dynamicptheadselection_pa_kernel(tc, qz, channel_u_w, channel_v_w, out)
             )
 
         lowest = keep.tile([P, HEADS, C_TILES, E_BANKS], F32, name="lowest")
-        sums = keep.tile([P, C_TILES, HEADS], F32, name="sums")
+        sums = keep.tile([P, C_TILES, HEADS + 1], F32, name="sums")
+        nc.vector.memset(sums[:], 0.5)
 
         def logit_banks(h, j):
             queries = slice(j * P, (j + 1) * P)
@@ -187,28 +189,31 @@ def tile_dynamicptheadselection_pa_kernel(tc, qz, channel_u_w, channel_v_w, out)
             )
 
         inverse = keep.tile([P, C_TILES, HEADS], F32, name="inverse")
-        ratio = keep.tile([P, C_TILES], F32, name="ratio")
-        half_inverse = keep.tile([P, C_TILES], F32, name="half_inverse")
+        coefficient = keep.tile([P, C_TILES, HEADS], F32, name="coefficient")
 
         def invert_sums(j):
-            nc.vector.reciprocal(out=inverse[:, j, :], in_=sums[:, j, :])
+            nc.vector.reciprocal(out=inverse[:, j, :], in_=sums[:, j, 0:HEADS])
 
         def coefficients(j):
-            nc.vector.tensor_tensor(out=ratio[:, j : j + 1], in0=sums[:, j, 1:2], in1=inverse[:, j, 0:1], op=ALU.mult)
-            nc.vector.tensor_scalar(
-                out=half_inverse[:, j : j + 1], in0=inverse[:, j, 1:2], scalar1=0.5, scalar2=None, op0=ALU.mult
+            nc.vector.tensor_tensor(
+                out=coefficient[:, j, :], in0=inverse[:, j, :], in1=sums[:, j, 1 : HEADS + 1], op=ALU.mult
             )
 
         def mix_heads(j, exp0, exp1):
             nc.vector.scalar_tensor_tensor(
-                out=exp1, in0=exp0, scalar=ratio[:, j : j + 1], in1=exp1, op0=ALU.mult, op1=ALU.add
+                out=exp1, in0=exp0, scalar=coefficient[:, j, 0:1], in1=exp1, op0=ALU.mult, op1=ALU.add
             )
 
-        def scale_and_store(j, mixed):
+        def scale_and_store(j, mixed, keys):
             nc.vector.scalar_tensor_tensor(
-                out=mixed, in0=mixed, scalar=half_inverse[:, j : j + 1], in1=x_rows[:, j, :], op0=ALU.mult, op1=ALU.mult
+                out=mixed[:, keys],
+                in0=mixed[:, keys],
+                scalar=coefficient[:, j, 1:2],
+                in1=x_rows[:, j, keys],
+                op0=ALU.mult,
+                op1=ALU.mult,
             )
-            nc.sync.dma_start(out=out_dram[:, j, :], in_=mixed)
+            nc.sync.dma_start(out=out_dram[:, j, keys], in_=mixed[:, keys])
 
         transpose_weights("v", 0, True)
         for pair in range(C_TILES // 2):
@@ -219,17 +224,17 @@ def tile_dynamicptheadselection_pa_kernel(tc, qz, channel_u_w, channel_v_w, out)
             else:
                 quantise_x_pair(pair - 1)
         project("v", 0, 0, False)
-        project("v", 0, 1, True)
+        project("v", 0, 1, False)
         quantise_x_pair(C_TILES // 2 - 1)
         project("v", 0, 2, False)
-        project("v", 0, 3, True)
+        project("v", 0, 3, False)
         transpose_weights("u", 0, True)
         quantise_projection("v", 0, 0, BANK)
         project("v", 0, 4, False)
-        project("v", 0, 5, True)
+        project("v", 0, 5, False)
         quantise_weights("u", 0)
         project("v", 0, 6, False)
-        project("v", 0, 7, True)
+        project("v", 0, 7, False)
 
         def project_queries(n):
             if n < HEADS * C_TILES:
@@ -247,6 +252,8 @@ def tile_dynamicptheadselection_pa_kernel(tc, qz, channel_u_w, channel_v_w, out)
         quantise_projection("v", 0, BANK, BANK)
         project_queries(1)
         quantise_queries(0)
+        project_queries(2)
+        quantise_queries(1)
 
         stages = (
             (lambda: transpose_weights("v", 1, False), lambda: quantise_weights("v", 1)),
@@ -258,32 +265,38 @@ def tile_dynamicptheadselection_pa_kernel(tc, qz, channel_u_w, channel_v_w, out)
         for j in range(C_TILES):
             four_banks, then_quantise = stages[j // 2]
             filled = logit_banks(0, j)
-            project_queries(j + 2)
+            project_queries(j + 3)
             if j % 2 == 0:
                 four_banks()
+            else:
+                exponentials(0, j // 2, exp_head0[:, j // 2, :])
             fold_bank(0, j, 0, filled[0], exp_head0[:, j, :])
-            quantise_queries(j + 1)
+            quantise_queries(j + 2)
             if j % 2 == 1:
                 then_quantise()
             fold_bank(0, j, 1, filled[1], exp_head0[:, j, :])
 
         exp_head1 = {}
-        for j in range(C_TILES + 1):
+        for j in range(C_TILES + LAG):
+            k = j - LAG
             if j < C_TILES:
                 exp_head1[j] = results.tile([P, C], F32, tag="exp_head1", name="exp_head1")
                 filled = logit_banks(1, j)
-                project_queries(C_TILES + j + 2)
-                exponentials(0, j, exp_head0[:, j, :])
+                project_queries(C_TILES + j + 3)
+                if j % 2 == 1:
+                    exponentials(0, (C_TILES + j) // 2, exp_head0[:, (C_TILES + j) // 2, :])
                 fold_bank(1, j, 0, filled[0], exp_head1[j][:])
-            if j > 0:
-                invert_sums(j - 1)
+            if k >= 0:
+                invert_sums(k)
             if j < C_TILES:
-                quantise_queries(C_TILES + j + 1)
-            if j > 0:
-                coefficients(j - 1)
-                mix_heads(j - 1, exp_head0[:, j - 1, :], exp_head1[j - 1][:])
+                quantise_queries(C_TILES + j + 2)
+            if k >= 0:
+                coefficients(k)
+                mix_heads(k, exp_head0[:, k, :], exp_head1[k][:])
             if j < C_TILES:
                 fold_bank(1, j, 1, filled[1], exp_head1[j][:])
                 exponentials(1, j, exp_head1[j][:])
-            if j > 0:
-                scale_and_store(j - 1, exp_head1[j - 1][:])
+            if 0 <= k < C_TILES - 1:
+                scale_and_store(k, exp_head1[k][:], slice(0, C))
+        for i in range(E_BANKS):
+            scale_and_store(C_TILES - 1, exp_head1[C_TILES - 1][:], slice(i * BANK, (i + 1) * BANK))

@@ -39,7 +39,6 @@ def tile_dynamicptheadselection_pa_kernel(tc, qz, channel_u_w, channel_v_w, out)
     }
 
     with ExitStack() as ctx:
-        ctx.enter_context(tc.manual_schedule())
         keep = ctx.enter_context(tc.tile_pool(name="keep", bufs=1))
         staging = ctx.enter_context(tc.tile_pool(name="staging", bufs=2))
         results = ctx.enter_context(tc.tile_pool(name="results", bufs=LAG + 3))

@@ -20,9 +20,13 @@ D = 1024
 HEADS = 2
 R = D // HEADS
 C_TILES = C // P
+C_PAIRS = C_TILES // 2
 D_PASSES = D // K_PASS
 BANK = 512
 E_BANKS = C // BANK
+QUERY_TILES = HEADS * C_TILES
+PROJECT_AHEAD = 3
+QUANTISE_AHEAD = 2
 LAG = 2
 
 FLOPS = 2 * C * D * (2 * D) + HEADS * 2 * C * C * R
@@ -39,6 +43,7 @@ def tile_dynamicptheadselection_pa_kernel(tc, qz, channel_u_w, channel_v_w, out)
     }
 
     with ExitStack() as ctx:
+        ctx.enter_context(tc.manual_schedule())
         keep = ctx.enter_context(tc.tile_pool(name="keep", bufs=1))
         staging = ctx.enter_context(tc.tile_pool(name="staging", bufs=2))
         results = ctx.enter_context(tc.tile_pool(name="results", bufs=LAG + 3))
@@ -66,12 +71,6 @@ def tile_dynamicptheadselection_pa_kernel(tc, qz, channel_u_w, channel_v_w, out)
         table_warmer = keep.tile([P, 1], F32, name="table_warmer")
         nc.scalar.activation(out=table_warmer[:], in_=identity[:, 0:1], func=EXP)
 
-        def copy_out(out_view, bank_view, on_vector):
-            if on_vector:
-                nc.vector.tensor_copy(out=out_view, in_=bank_view)
-            else:
-                nc.scalar.copy(out=out_view, in_=bank_view)
-
         def quantise(grouped, codes, scales):
             nc.vector.quantize_mx(out=codes.bitcast(FP8X4), scales=scales, in_=grouped)
 
@@ -81,11 +80,12 @@ def tile_dynamicptheadselection_pa_kernel(tc, qz, channel_u_w, channel_v_w, out)
             for k in range(2 * D_PASSES):
                 nc.tensor.transpose(bank[:, k, :], words[:, k * P : (k + 1) * P], identity[:])
             grouped_words = grouped.bitcast(F32).rearrange("p g (c u) -> p g c u", u=2)
-            copy_out(
-                grouped_words[:, :, first_column : first_column + P, :],
-                bank[:].rearrange("p (g u) c -> p g c u", u=2),
-                on_vector,
-            )
+            target = grouped_words[:, :, first_column : first_column + P, :]
+            source = bank[:].rearrange("p (g u) c -> p g c u", u=2)
+            if on_vector:
+                nc.vector.tensor_copy(out=target, in_=source)
+            else:
+                nc.scalar.copy(out=target, in_=source)
 
         x_grouped = keep.tile([P, D_PASSES, C * PACK], BF16, name="x_grouped", align_bytes=64)
         x_codes = keep.tile([P, D_PASSES, C], U32, name="x_codes", align_bytes=64)
@@ -96,6 +96,10 @@ def tile_dynamicptheadselection_pa_kernel(tc, qz, channel_u_w, channel_v_w, out)
         q_grouped = {}
         q_codes = {}
         q_scales = {}
+
+        def transpose_x_pair(pair):
+            transpose_row_tile(x_rows[:, 2 * pair, :], x_grouped[:], 2 * pair * P, False)
+            transpose_row_tile(x_rows[:, 2 * pair + 1, :], x_grouped[:], (2 * pair + 1) * P, True)
 
         def quantise_x_pair(pair):
             channels = slice(2 * pair * P, 2 * (pair + 1) * P)
@@ -119,7 +123,7 @@ def tile_dynamicptheadselection_pa_kernel(tc, qz, channel_u_w, channel_v_w, out)
             q_codes[w, h] = keep.tile([P, C], U32, name="q%s%d_codes" % (w, h), align_bytes=64)
             q_scales[w, h] = keep.tile([P, C], U8, name="q%s%d_scales" % (w, h), align_bytes=64)
 
-        def project(w, h, j, on_vector):
+        def project(w, h, j):
             channels = slice(j * P, (j + 1) * P)
             bank = banks.tile([P, PACK, P], F32, tag="bank", name="projected")
             for t in range(PACK):
@@ -134,7 +138,7 @@ def tile_dynamicptheadselection_pa_kernel(tc, qz, channel_u_w, channel_v_w, out)
                         start=(g == 0),
                         stop=(g == D_PASSES - 1),
                     )
-            copy_out(q_grouped[w, h][:, channels, :], bank[:].rearrange("p t c -> p c t"), on_vector)
+            nc.scalar.copy(out=q_grouped[w, h][:, channels, :], in_=bank[:].rearrange("p t c -> p c t"))
 
         def quantise_projection(w, h, first, count):
             channels = slice(first, first + count)
@@ -143,6 +147,21 @@ def tile_dynamicptheadselection_pa_kernel(tc, qz, channel_u_w, channel_v_w, out)
                 q_codes[w, h][:, channels],
                 q_scales[w, h][:, channels],
             )
+
+        def project_key_pair(h, pair):
+            project("v", h, 2 * pair)
+            project("v", h, 2 * pair + 1)
+
+        def quantise_keys(h, i):
+            quantise_projection("v", h, i * BANK, BANK)
+
+        def project_queries(n):
+            if n < QUERY_TILES:
+                project("u", n // C_TILES, n % C_TILES)
+
+        def quantise_queries(n):
+            if n < QUERY_TILES:
+                quantise_projection("u", n // C_TILES, (n % C_TILES) * P, P)
 
         lowest = keep.tile([P, HEADS, C_TILES, E_BANKS], F32, name="lowest")
         sums = keep.tile([P, C_TILES, HEADS + 1], F32, name="sums")
@@ -215,82 +234,68 @@ def tile_dynamicptheadselection_pa_kernel(tc, qz, channel_u_w, channel_v_w, out)
             nc.sync.dma_start(out=out_dram[:, j, keys], in_=mixed[:, keys])
 
         transpose_weights("v", 0, True)
-        for pair in range(C_TILES // 2):
-            transpose_row_tile(x_rows[:, 2 * pair, :], x_grouped[:], 2 * pair * P, False)
-            transpose_row_tile(x_rows[:, 2 * pair + 1, :], x_grouped[:], (2 * pair + 1) * P, True)
-            if pair == 0:
-                quantise_weights("v", 0)
-            else:
-                quantise_x_pair(pair - 1)
-        project("v", 0, 0, False)
-        project("v", 0, 1, False)
-        quantise_x_pair(C_TILES // 2 - 1)
-        project("v", 0, 2, False)
-        project("v", 0, 3, False)
+        transpose_x_pair(0)
+        quantise_weights("v", 0)
+        for pair in range(1, C_PAIRS):
+            transpose_x_pair(pair)
+            quantise_x_pair(pair - 1)
+        project_key_pair(0, 0)
+        quantise_x_pair(C_PAIRS - 1)
+        project_key_pair(0, 1)
         transpose_weights("u", 0, True)
-        quantise_projection("v", 0, 0, BANK)
-        project("v", 0, 4, False)
-        project("v", 0, 5, False)
+        quantise_keys(0, 0)
+        project_key_pair(0, 2)
         quantise_weights("u", 0)
-        project("v", 0, 6, False)
-        project("v", 0, 7, False)
-
-        def project_queries(n):
-            if n < HEADS * C_TILES:
-                project("u", n // C_TILES, n % C_TILES, False)
-
-        def quantise_queries(n):
-            if n < HEADS * C_TILES:
-                quantise_projection("u", n // C_TILES, (n % C_TILES) * P, P)
-
-        def project_keys(h, i):
-            for j in range(i * PACK, (i + 1) * PACK):
-                project("v", h, j, False)
-
+        project_key_pair(0, 3)
         project_queries(0)
-        quantise_projection("v", 0, BANK, BANK)
-        project_queries(1)
-        quantise_queries(0)
-        project_queries(2)
-        quantise_queries(1)
+        quantise_keys(0, 1)
+        for n in range(1, PROJECT_AHEAD):
+            project_queries(n)
+            quantise_queries(n - 1)
+
+        def project_four_key_tiles(i):
+            project_key_pair(1, 2 * i)
+            project_key_pair(1, 2 * i + 1)
 
         stages = (
             (lambda: transpose_weights("v", 1, False), lambda: quantise_weights("v", 1)),
             (lambda: transpose_weights("u", 1, False), lambda: quantise_weights("u", 1)),
-            (lambda: project_keys(1, 0), lambda: quantise_projection("v", 1, 0, BANK)),
-            (lambda: project_keys(1, 1), lambda: quantise_projection("v", 1, BANK, BANK)),
+            (lambda: project_four_key_tiles(0), lambda: quantise_keys(1, 0)),
+            (lambda: project_four_key_tiles(1), lambda: quantise_keys(1, 1)),
         )
         exp_head0 = keep.tile([P, C_TILES, C], F32, name="exp_head0")
-        for j in range(C_TILES):
-            four_banks, then_quantise = stages[j // 2]
-            filled = logit_banks(0, j)
-            project_queries(j + 3)
-            if j % 2 == 0:
+        for n in range(C_TILES):
+            four_banks, then_quantise = stages[n // 2]
+            filled = logit_banks(0, n)
+            project_queries(n + PROJECT_AHEAD)
+            if n % 2 == 0:
                 four_banks()
             else:
-                exponentials(0, j // 2, exp_head0[:, j // 2, :])
-            fold_bank(0, j, 0, filled[0], exp_head0[:, j, :])
-            quantise_queries(j + 2)
-            if j % 2 == 1:
+                exponentials(0, n // 2, exp_head0[:, n // 2, :])
+            fold_bank(0, n, 0, filled[0], exp_head0[:, n, :])
+            quantise_queries(n + QUANTISE_AHEAD)
+            if n % 2 == 1:
                 then_quantise()
-            fold_bank(0, j, 1, filled[1], exp_head0[:, j, :])
+            fold_bank(0, n, 1, filled[1], exp_head0[:, n, :])
 
         exp_head1 = {}
         for j in range(C_TILES + LAG):
+            n = C_TILES + j
             k = j - LAG
-            if j < C_TILES:
-                exp_head1[j] = results.tile([P, C], F32, tag="exp_head1", name="exp_head1")
-                filled = logit_banks(1, j)
-                project_queries(C_TILES + j + 3)
-                if j % 2 == 1:
-                    exponentials(0, (C_TILES + j) // 2, exp_head0[:, (C_TILES + j) // 2, :])
-                fold_bank(1, j, 0, filled[0], exp_head1[j][:])
             if k >= 0:
                 invert_sums(k)
             if j < C_TILES:
-                quantise_queries(C_TILES + j + 2)
+                exp_head1[j] = results.tile([P, C], F32, tag="exp_head1", name="exp_head1")
+                filled = logit_banks(1, j)
+                project_queries(n + PROJECT_AHEAD)
+                if n % 2 == 1:
+                    exponentials(0, n // 2, exp_head0[:, n // 2, :])
+                fold_bank(1, j, 0, filled[0], exp_head1[j][:])
             if k >= 0:
                 coefficients(k)
+            if j < C_TILES:
+                quantise_queries(n + QUANTISE_AHEAD)
+            if k >= 0:
                 mix_heads(k, exp_head0[:, k, :], exp_head1[k][:])
             if j < C_TILES:
                 fold_bank(1, j, 1, filled[1], exp_head1[j][:])

@@ -11,6 +11,7 @@ U8 = mybir.dt.uint8
 FP8X4 = mybir.dt.float8_e4m3fn_x4
 ALU = mybir.AluOpType
 EXP = mybir.ActivationFunctionType.Exp
+COPY = mybir.ActivationFunctionType.Copy
 
 P = 128
 PACK = 4
@@ -20,7 +21,6 @@ D = 1024
 HEADS = 2
 R = D // HEADS
 C_TILES = C // P
-C_PAIRS = C_TILES // 2
 D_PASSES = D // K_PASS
 BANK = 512
 E_BANKS = C // BANK
@@ -28,6 +28,8 @@ QUERY_TILES = HEADS * C_TILES
 PROJECT_AHEAD = 3
 QUANTISE_AHEAD = 2
 LAG = 2
+TENSOR_FROM = 640
+TENSOR_TILES = C_TILES - 1
 
 FLOPS = 2 * C * D * (2 * D) + HEADS * 2 * C * C * R
 
@@ -45,9 +47,20 @@ def tile_dynamicptheadselection_pa_kernel(tc, qz, channel_u_w, channel_v_w, out)
     with ExitStack() as ctx:
         ctx.enter_context(tc.manual_schedule())
         keep = ctx.enter_context(tc.tile_pool(name="keep", bufs=1))
-        staging = ctx.enter_context(tc.tile_pool(name="staging", bufs=2))
-        results = ctx.enter_context(tc.tile_pool(name="results", bufs=LAG + 3))
-        banks = ctx.enter_context(tc.psum_pool(name="banks", bufs=8))
+        staging = ctx.enter_context(tc.tile_pool(name="staging", bufs=3))
+        results = ctx.enter_context(tc.tile_pool(name="results", bufs=LAG + 4))
+        queries = ctx.enter_context(tc.tile_pool(name="queries", bufs=4))
+        diagonals = ctx.enter_context(tc.tile_pool(name="diagonals", bufs=4))
+        logit_pool = ctx.enter_context(tc.psum_pool(name="logit_pool", bufs=4))
+        work_pool = ctx.enter_context(tc.psum_pool(name="work_pool", bufs=4))
+        spare_logit_banks = [True, True]
+
+        def work_bank(shape, name):
+            use_logit_bank = spare_logit_banks[0] and spare_logit_banks[1]
+            spare_logit_banks[1] = not spare_logit_banks[1]
+            if use_logit_bank:
+                return logit_pool.tile(shape, F32, tag="logits", name=name)
+            return work_pool.tile(shape, F32, tag="work", name=name)
 
         x_rows = keep.tile([P, C_TILES, D], BF16, name="x_rows")
         w_rows = {}
@@ -55,37 +68,44 @@ def tile_dynamicptheadselection_pa_kernel(tc, qz, channel_u_w, channel_v_w, out)
             for w in ("v", "u"):
                 w_rows[w, h] = keep.tile([P, PACK, D], BF16, name="%s%d_rows" % (w, h))
 
-        def load_weights(w, h):
-            for t in range(0, PACK, 2):
-                nc.sync.dma_start(out=w_rows[w, h][:, t : t + 2, :], in_=w_dram[w][h, :, t : t + 2, :])
+        def load_weights(w, h, count):
+            for t in range(0, PACK, count):
+                nc.sync.dma_start(out=w_rows[w, h][:, t : t + count, :], in_=w_dram[w][h, :, t : t + count, :])
 
-        load_weights("v", 0)
-        for j in range(0, C_TILES, 2):
-            nc.sync.dma_start(out=x_rows[:, j : j + 2, :], in_=x_dram[:, j : j + 2, :])
-        load_weights("u", 0)
-        load_weights("v", 1)
-        load_weights("u", 1)
+        load_weights("v", 0, 1)
+        for j in range(C_TILES):
+            nc.sync.dma_start(out=x_rows[:, j, :], in_=x_dram[:, j, :])
+        load_weights("u", 0, 2)
+        load_weights("u", 1, 2)
+        load_weights("v", 1, 2)
 
         identity = keep.tile([P, P], F32, name="identity")
         make_identity(nc, identity[:])
         table_warmer = keep.tile([P, 1], F32, name="table_warmer")
         nc.scalar.activation(out=table_warmer[:], in_=identity[:, 0:1], func=EXP)
+        half_identity = keep.tile([P, P], F32, name="half_identity")
+        nc.scalar.activation(out=half_identity[:], in_=identity[:], func=COPY, scale=0.5)
+
+        def copy_out(on_vector, out, in_):
+            if on_vector:
+                nc.vector.tensor_copy(out=out, in_=in_)
+            else:
+                nc.scalar.copy(out=out, in_=in_)
 
         def quantise(grouped, codes, scales):
             nc.vector.quantize_mx(out=codes.bitcast(FP8X4), scales=scales, in_=grouped)
 
         def transpose_row_tile(rows, grouped, first_column, on_vector):
             words = rows.bitcast(F32)
-            bank = banks.tile([P, 2 * D_PASSES, P], F32, tag="bank", name="transposed")
+            bank = work_bank([P, 2 * D_PASSES, P], "transposed")
             for k in range(2 * D_PASSES):
                 nc.tensor.transpose(bank[:, k, :], words[:, k * P : (k + 1) * P], identity[:])
             grouped_words = grouped.bitcast(F32).rearrange("p g (c u) -> p g c u", u=2)
-            target = grouped_words[:, :, first_column : first_column + P, :]
-            source = bank[:].rearrange("p (g u) c -> p g c u", u=2)
-            if on_vector:
-                nc.vector.tensor_copy(out=target, in_=source)
-            else:
-                nc.scalar.copy(out=target, in_=source)
+            copy_out(
+                on_vector,
+                grouped_words[:, :, first_column : first_column + P, :],
+                bank[:].rearrange("p (g u) c -> p g c u", u=2),
+            )
 
         x_grouped = keep.tile([P, D_PASSES, C * PACK], BF16, name="x_grouped", align_bytes=64)
         x_codes = keep.tile([P, D_PASSES, C], U32, name="x_codes", align_bytes=64)
@@ -97,9 +117,8 @@ def tile_dynamicptheadselection_pa_kernel(tc, qz, channel_u_w, channel_v_w, out)
         q_codes = {}
         q_scales = {}
 
-        def transpose_x_pair(pair):
-            transpose_row_tile(x_rows[:, 2 * pair, :], x_grouped[:], 2 * pair * P, False)
-            transpose_row_tile(x_rows[:, 2 * pair + 1, :], x_grouped[:], (2 * pair + 1) * P, True)
+        def transpose_x(j, on_vector):
+            transpose_row_tile(x_rows[:, j, :], x_grouped[:], j * P, on_vector)
 
         def quantise_x_pair(pair):
             channels = slice(2 * pair * P, 2 * (pair + 1) * P)
@@ -107,25 +126,28 @@ def tile_dynamicptheadselection_pa_kernel(tc, qz, channel_u_w, channel_v_w, out)
             for g in range(D_PASSES):
                 quantise(x_grouped[:, g, values], x_codes[:, g, channels], x_scales[:, g, channels])
 
-        def transpose_weights(w, h, share_with_vector):
+        def transpose_weights(w, h, vector_tiles, between=None):
             w_grouped[w, h] = staging.tile(
                 [P, D_PASSES, R * PACK], BF16, tag="w_grouped", name="w_grouped", align_bytes=64
             )
             for t in range(PACK):
-                transpose_row_tile(w_rows[w, h][:, t, :], w_grouped[w, h][:], t * P, share_with_vector and t % 2 == 1)
+                if between is not None and t == PACK - 1:
+                    between()
+                transpose_row_tile(w_rows[w, h][:, t, :], w_grouped[w, h][:], t * P, t in vector_tiles)
 
         def quantise_weights(w, h):
             w_codes[w, h] = keep.tile([P, D_PASSES, R], U32, name="%s%d_codes" % (w, h), align_bytes=64)
             w_scales[w, h] = keep.tile([P, D_PASSES, R], U8, name="%s%d_scales" % (w, h), align_bytes=64)
             for g in range(D_PASSES):
                 quantise(w_grouped[w, h][:, g, :], w_codes[w, h][:, g, :], w_scales[w, h][:, g, :])
-            q_grouped[w, h] = keep.tile([P, C, PACK], BF16, name="q%s%d_grouped" % (w, h), align_bytes=64)
+            if w == "v":
+                q_grouped[w, h] = keep.tile([P, C, PACK], BF16, name="q%s%d_grouped" % (w, h), align_bytes=64)
             q_codes[w, h] = keep.tile([P, C], U32, name="q%s%d_codes" % (w, h), align_bytes=64)
             q_scales[w, h] = keep.tile([P, C], U8, name="q%s%d_scales" % (w, h), align_bytes=64)
 
-        def project(w, h, j):
+        def project(w, h, j, target, on_vector):
             channels = slice(j * P, (j + 1) * P)
-            bank = banks.tile([P, PACK, P], F32, tag="bank", name="projected")
+            bank = work_bank([P, PACK, P], "projected")
             for t in range(PACK):
                 rows_t = slice(t * P, (t + 1) * P)
                 for g in range(D_PASSES):
@@ -138,57 +160,64 @@ def tile_dynamicptheadselection_pa_kernel(tc, qz, channel_u_w, channel_v_w, out)
                         start=(g == 0),
                         stop=(g == D_PASSES - 1),
                     )
-            nc.scalar.copy(out=q_grouped[w, h][:, channels, :], in_=bank[:].rearrange("p t c -> p c t"))
+            copy_out(on_vector, target, bank[:].rearrange("p t c -> p c t"))
 
-        def quantise_projection(w, h, first, count):
+        def quantise_projection(w, h, grouped, first, count):
             channels = slice(first, first + count)
-            quantise(
-                q_grouped[w, h][:, channels, :].rearrange("p c t -> p (c t)"),
-                q_codes[w, h][:, channels],
-                q_scales[w, h][:, channels],
-            )
+            quantise(grouped.rearrange("p c t -> p (c t)"), q_codes[w, h][:, channels], q_scales[w, h][:, channels])
 
-        def project_key_pair(h, pair):
-            project("v", h, 2 * pair)
-            project("v", h, 2 * pair + 1)
+        def project_keys(h, j, on_vector=False):
+            project("v", h, j, q_grouped["v", h][:, j * P : (j + 1) * P, :], on_vector)
 
         def quantise_keys(h, i):
-            quantise_projection("v", h, i * BANK, BANK)
+            quantise_projection("v", h, q_grouped["v", h][:, i * BANK : (i + 1) * BANK, :], i * BANK, BANK)
 
         def project_queries(n):
             if n < QUERY_TILES:
-                project("u", n // C_TILES, n % C_TILES)
+                h, j = divmod(n, C_TILES)
+                q_grouped["u", h, j] = queries.tile([P, P, PACK], BF16, tag="queries", name="queries", align_bytes=64)
+                project("u", h, j, q_grouped["u", h, j][:], False)
 
         def quantise_queries(n):
             if n < QUERY_TILES:
-                quantise_projection("u", n // C_TILES, (n % C_TILES) * P, P)
+                h, j = divmod(n, C_TILES)
+                quantise_projection("u", h, q_grouped["u", h, j][:], j * P, P)
 
         lowest = keep.tile([P, HEADS, C_TILES, E_BANKS], F32, name="lowest")
         sums = keep.tile([P, C_TILES, HEADS + 1], F32, name="sums")
         nc.vector.memset(sums[:], 0.5)
+        exp_head0 = keep.tile([P, C_TILES, C], F32, name="exp_head0")
+        exp_head1 = {}
 
-        def logit_banks(h, j):
-            queries = slice(j * P, (j + 1) * P)
-            filled = []
-            for i in range(E_BANKS):
-                keys = slice(i * BANK, (i + 1) * BANK)
-                bank = banks.tile([P, BANK], F32, tag="bank", name="logit_bank")
-                nc.tensor.matmul_mx(
-                    out=bank[:],
-                    lhsT=q_codes["u", h][:, queries].bitcast(FP8X4),
-                    lhsT_scale=q_scales["u", h][:, queries],
-                    rhs=q_codes["v", h][:, keys].bitcast(FP8X4),
-                    rhs_scale=q_scales["v", h][:, keys],
-                    start=True,
-                    stop=True,
-                )
-                filled.append(bank)
-            return filled
+        def exps(h, j):
+            return exp_head0[:, j, :] if h == 0 else exp_head1[j][:]
 
-        def fold_bank(h, j, i, bank, negated):
+        filled = {}
+
+        def logit_banks(n):
+            if n < QUERY_TILES:
+                h, j = divmod(n, C_TILES)
+                rows = slice(j * P, (j + 1) * P)
+                for i in range(E_BANKS):
+                    keys = slice(i * BANK, (i + 1) * BANK)
+                    filled[n, i] = logit_pool.tile([P, BANK], F32, tag="logits", name="logit_bank")
+                    nc.tensor.matmul_mx(
+                        out=filled[n, i][:],
+                        lhsT=q_codes["u", h][:, rows].bitcast(FP8X4),
+                        lhsT_scale=q_scales["u", h][:, rows],
+                        rhs=q_codes["v", h][:, keys].bitcast(FP8X4),
+                        rhs_scale=q_scales["v", h][:, keys],
+                        start=True,
+                        stop=True,
+                    )
+
+        def fold_bank(n, i):
+            h, j = divmod(n, C_TILES)
+            if h == 1 and i == 0:
+                exp_head1[j] = results.tile([P, C], F32, tag="exp_head1", name="exp_head1")
             nc.vector.tensor_scalar(
-                out=negated[:, i * BANK : (i + 1) * BANK],
-                in0=bank[:],
+                out=exps(h, j)[:, i * BANK : (i + 1) * BANK],
+                in0=filled[n, i][:],
                 scalar1=-1.0 / math.sqrt(R),
                 scalar2=(None if i == 0 else lowest[:, h, j, i - 1 : i]),
                 op0=ALU.mult,
@@ -196,10 +225,10 @@ def tile_dynamicptheadselection_pa_kernel(tc, qz, channel_u_w, channel_v_w, out)
                 accum_out=lowest[:, h, j, i : i + 1],
             )
 
-        def exponentials(h, j, negated):
+        def exponentials(h, j):
             nc.scalar.activation(
-                out=negated,
-                in_=negated,
+                out=exps(h, j),
+                in_=exps(h, j),
                 func=EXP,
                 bias=lowest[:, h, j, E_BANKS - 1 : E_BANKS],
                 scale=-1.0,
@@ -208,99 +237,146 @@ def tile_dynamicptheadselection_pa_kernel(tc, qz, channel_u_w, channel_v_w, out)
 
         inverse = keep.tile([P, C_TILES, HEADS], F32, name="inverse")
         coefficient = keep.tile([P, C_TILES, HEADS], F32, name="coefficient")
+        tensor_columns = slice(TENSOR_FROM, C)
+        mixed_bank = {}
+        diagonal = {}
+
+        def vector_columns(j):
+            return slice(0, TENSOR_FROM if j < TENSOR_TILES else C)
+
+        def store(j, keys):
+            nc.sync.dma_start(out=out_dram[:, j, keys], in_=exps(1, j)[:, keys])
 
         def invert_sums(j):
             nc.vector.reciprocal(out=inverse[:, j, :], in_=sums[:, j, 0:HEADS])
+            if j < TENSOR_TILES:
+                for h in range(HEADS):
+                    diagonal[h, j] = diagonals.tile([P, P], F32, tag="diagonal", name="diagonal")
+                    nc.scalar.activation(
+                        out=diagonal[h, j][:], in_=half_identity[:], func=COPY, scale=inverse[:, j, h : h + 1]
+                    )
+
+        def tensor_mix(j):
+            mixed_bank[j] = work_bank([P, C - TENSOR_FROM], "mixed")
+            for h in range(HEADS):
+                nc.tensor.matmul(
+                    out=mixed_bank[j][:],
+                    lhsT=diagonal[h, j][:],
+                    rhs=exps(h, j)[:, tensor_columns],
+                    start=(h == 0),
+                    stop=(h == HEADS - 1),
+                )
+
+        def finish_tensor_columns(j):
+            nc.vector.tensor_tensor(
+                out=exps(1, j)[:, tensor_columns],
+                in0=mixed_bank[j][:],
+                in1=x_rows[:, j, tensor_columns],
+                op=ALU.mult,
+            )
+            store(j, tensor_columns)
 
         def coefficients(j):
             nc.vector.tensor_tensor(
                 out=coefficient[:, j, :], in0=inverse[:, j, :], in1=sums[:, j, 1 : HEADS + 1], op=ALU.mult
             )
 
-        def mix_heads(j, exp0, exp1):
+        def vector_mix(j):
+            keys = vector_columns(j)
             nc.vector.scalar_tensor_tensor(
-                out=exp1, in0=exp0, scalar=coefficient[:, j, 0:1], in1=exp1, op0=ALU.mult, op1=ALU.add
+                out=exps(1, j)[:, keys],
+                in0=exps(0, j)[:, keys],
+                scalar=coefficient[:, j, 0:1],
+                in1=exps(1, j)[:, keys],
+                op0=ALU.mult,
+                op1=ALU.add,
             )
 
-        def scale_and_store(j, mixed, keys):
+        def finish_vector_columns(j, keys):
             nc.vector.scalar_tensor_tensor(
-                out=mixed[:, keys],
-                in0=mixed[:, keys],
+                out=exps(1, j)[:, keys],
+                in0=exps(1, j)[:, keys],
                 scalar=coefficient[:, j, 1:2],
                 in1=x_rows[:, j, keys],
                 op0=ALU.mult,
                 op1=ALU.mult,
             )
-            nc.sync.dma_start(out=out_dram[:, j, keys], in_=mixed[:, keys])
+            store(j, keys)
 
-        transpose_weights("v", 0, True)
-        transpose_x_pair(0)
+        transpose_weights("v", 0, (1,))
+        transpose_x(0, False)
+        transpose_x(1, False)
         quantise_weights("v", 0)
-        for pair in range(1, C_PAIRS):
-            transpose_x_pair(pair)
-            quantise_x_pair(pair - 1)
-        project_key_pair(0, 0)
-        quantise_x_pair(C_PAIRS - 1)
-        project_key_pair(0, 1)
-        transpose_weights("u", 0, True)
+        transpose_x(2, False)
+        transpose_x(3, False)
+        quantise_x_pair(0)
+        transpose_x(4, True)
+        transpose_x(5, True)
+        quantise_x_pair(1)
+        for j in range(4):
+            project_keys(0, j, j == 2)
+        quantise_x_pair(2)
+        transpose_x(6, True)
+        transpose_x(7, False)
+        transpose_weights("u", 0, (0, 2))
         quantise_keys(0, 0)
-        project_key_pair(0, 2)
-        quantise_weights("u", 0)
-        project_key_pair(0, 3)
+        quantise_x_pair(3)
+        transpose_weights("u", 1, (3,), lambda: quantise_weights("u", 0))
+        transpose_weights("v", 1, (1, 3))
+        quantise_weights("u", 1)
+        for j in range(4, 8):
+            project_keys(0, j)
         project_queries(0)
+        project_queries(1)
+        quantise_weights("v", 1)
         quantise_keys(0, 1)
-        for n in range(1, PROJECT_AHEAD):
-            project_queries(n)
-            quantise_queries(n - 1)
+        quantise_queries(0)
+        project_queries(2)
+        quantise_queries(1)
+        spare_logit_banks[0] = False
+        project_keys(1, 0)
+        logit_banks(0)
 
-        def project_four_key_tiles(i):
-            project_key_pair(1, 2 * i)
-            project_key_pair(1, 2 * i + 1)
-
-        stages = (
-            (lambda: transpose_weights("v", 1, False), lambda: quantise_weights("v", 1)),
-            (lambda: transpose_weights("u", 1, False), lambda: quantise_weights("u", 1)),
-            (lambda: project_four_key_tiles(0), lambda: quantise_keys(1, 0)),
-            (lambda: project_four_key_tiles(1), lambda: quantise_keys(1, 1)),
-        )
-        exp_head0 = keep.tile([P, C_TILES, C], F32, name="exp_head0")
         for n in range(C_TILES):
-            four_banks, then_quantise = stages[n // 2]
-            filled = logit_banks(0, n)
+            fold_bank(n, 0)
             project_queries(n + PROJECT_AHEAD)
-            if n % 2 == 0:
-                four_banks()
-            else:
-                exponentials(0, n // 2, exp_head0[:, n // 2, :])
-            fold_bank(0, n, 0, filled[0], exp_head0[:, n, :])
+            if n + 1 < C_TILES:
+                project_keys(1, n + 1)
             quantise_queries(n + QUANTISE_AHEAD)
+            if n == C_TILES // 2:
+                quantise_keys(1, 0)
+            if n == C_TILES - 1:
+                quantise_keys(1, 1)
+            logit_banks(n + 1)
+            fold_bank(n, 1)
             if n % 2 == 1:
-                then_quantise()
-            fold_bank(0, n, 1, filled[1], exp_head0[:, n, :])
+                exponentials(0, n // 2)
 
-        exp_head1 = {}
-        for j in range(C_TILES + LAG):
+        for j in range(C_TILES + LAG + 1):
             n = C_TILES + j
             k = j - LAG
-            if k >= 0:
-                invert_sums(k)
             if j < C_TILES:
-                exp_head1[j] = results.tile([P, C], F32, tag="exp_head1", name="exp_head1")
-                filled = logit_banks(1, j)
+                fold_bank(n, 0)
                 project_queries(n + PROJECT_AHEAD)
-                if n % 2 == 1:
-                    exponentials(0, n // 2, exp_head0[:, n // 2, :])
-                fold_bank(1, j, 0, filled[0], exp_head1[j][:])
-            if k >= 0:
+                logit_banks(n + 1)
+            if 0 <= k < TENSOR_TILES:
+                tensor_mix(k)
+            if 2 <= j < 2 + C_TILES // 2:
+                exponentials(0, C_TILES // 2 + j - 2)
+            if 0 <= k < C_TILES:
                 coefficients(k)
             if j < C_TILES:
                 quantise_queries(n + QUANTISE_AHEAD)
-            if k >= 0:
-                mix_heads(k, exp_head0[:, k, :], exp_head1[k][:])
+            if 0 <= k - 1 < TENSOR_TILES:
+                finish_tensor_columns(k - 1)
+            if 0 <= k < C_TILES:
+                vector_mix(k)
             if j < C_TILES:
-                fold_bank(1, j, 1, filled[1], exp_head1[j][:])
-                exponentials(1, j, exp_head1[j][:])
+                fold_bank(n, 1)
+                exponentials(1, j)
+            if 0 <= k + 1 < C_TILES:
+                invert_sums(k + 1)
             if 0 <= k < C_TILES - 1:
-                scale_and_store(k, exp_head1[k][:], slice(0, C))
+                finish_vector_columns(k, vector_columns(k))
         for i in range(E_BANKS):
-            scale_and_store(C_TILES - 1, exp_head1[C_TILES - 1][:], slice(i * BANK, (i + 1) * BANK))
+            finish_vector_columns(C_TILES - 1, slice(i * BANK, (i + 1) * BANK))

@@ -28,7 +28,7 @@ QUERY_TILES = HEADS * C_TILES
 PROJECT_AHEAD = 3
 QUANTISE_AHEAD = 2
 LAG = 2
-TENSOR_FROM = 640
+TENSOR_FROM = BANK
 TENSOR_TILES = C_TILES - 1
 
 FLOPS = 2 * C * D * (2 * D) + HEADS * 2 * C * C * R
@@ -83,8 +83,6 @@ def tile_dynamicptheadselection_pa_kernel(tc, qz, channel_u_w, channel_v_w, out)
         make_identity(nc, identity[:])
         table_warmer = keep.tile([P, 1], F32, name="table_warmer")
         nc.scalar.activation(out=table_warmer[:], in_=identity[:, 0:1], func=EXP)
-        half_identity = keep.tile([P, P], F32, name="half_identity")
-        nc.scalar.activation(out=half_identity[:], in_=identity[:], func=COPY, scale=0.5)
 
         def copy_out(on_vector, out, in_):
             if on_vector:
@@ -244,42 +242,39 @@ def tile_dynamicptheadselection_pa_kernel(tc, qz, channel_u_w, channel_v_w, out)
         def vector_columns(j):
             return slice(0, TENSOR_FROM if j < TENSOR_TILES else C)
 
-        def store(j, keys):
-            nc.sync.dma_start(out=out_dram[:, j, keys], in_=exps(1, j)[:, keys])
-
         def invert_sums(j):
             nc.vector.reciprocal(out=inverse[:, j, :], in_=sums[:, j, 0:HEADS])
-            if j < TENSOR_TILES:
-                for h in range(HEADS):
-                    diagonal[h, j] = diagonals.tile([P, P], F32, tag="diagonal", name="diagonal")
-                    nc.scalar.activation(
-                        out=diagonal[h, j][:], in_=half_identity[:], func=COPY, scale=inverse[:, j, h : h + 1]
-                    )
 
         def tensor_mix(j):
             mixed_bank[j] = work_bank([P, C - TENSOR_FROM], "mixed")
-            for h in range(HEADS):
-                nc.tensor.matmul(
-                    out=mixed_bank[j][:],
-                    lhsT=diagonal[h, j][:],
-                    rhs=exps(h, j)[:, tensor_columns],
-                    start=(h == 0),
-                    stop=(h == HEADS - 1),
-                )
+            nc.tensor.matmul(
+                out=mixed_bank[j][:], lhsT=identity[:], rhs=exps(1, j)[:, tensor_columns], start=True, stop=False
+            )
+            nc.tensor.matmul(
+                out=mixed_bank[j][:], lhsT=diagonal[j][:], rhs=exps(0, j)[:, tensor_columns], start=False, stop=True
+            )
+
+        def finish_columns(j, keys, mixed):
+            nc.vector.scalar_tensor_tensor(
+                out=exps(1, j)[:, keys],
+                in0=mixed,
+                scalar=coefficient[:, j, 1:2],
+                in1=x_rows[:, j, keys],
+                op0=ALU.mult,
+                op1=ALU.mult,
+            )
+            nc.sync.dma_start(out=out_dram[:, j, keys], in_=exps(1, j)[:, keys])
 
         def finish_tensor_columns(j):
-            nc.vector.tensor_tensor(
-                out=exps(1, j)[:, tensor_columns],
-                in0=mixed_bank[j][:],
-                in1=x_rows[:, j, tensor_columns],
-                op=ALU.mult,
-            )
-            store(j, tensor_columns)
+            finish_columns(j, tensor_columns, mixed_bank[j][:])
 
         def coefficients(j):
             nc.vector.tensor_tensor(
                 out=coefficient[:, j, :], in0=inverse[:, j, :], in1=sums[:, j, 1 : HEADS + 1], op=ALU.mult
             )
+            if j < TENSOR_TILES:
+                diagonal[j] = diagonals.tile([P, P], F32, tag="diagonal", name="diagonal")
+                nc.scalar.activation(out=diagonal[j][:], in_=identity[:], func=COPY, scale=coefficient[:, j, 0:1])
 
         def vector_mix(j):
             keys = vector_columns(j)
@@ -293,15 +288,7 @@ def tile_dynamicptheadselection_pa_kernel(tc, qz, channel_u_w, channel_v_w, out)
             )
 
         def finish_vector_columns(j, keys):
-            nc.vector.scalar_tensor_tensor(
-                out=exps(1, j)[:, keys],
-                in0=exps(1, j)[:, keys],
-                scalar=coefficient[:, j, 1:2],
-                in1=x_rows[:, j, keys],
-                op0=ALU.mult,
-                op1=ALU.mult,
-            )
-            store(j, keys)
+            finish_columns(j, keys, exps(1, j)[:, keys])
 
         transpose_weights("v", 0, (1,))
         transpose_x(0, False)
@@ -363,8 +350,6 @@ def tile_dynamicptheadselection_pa_kernel(tc, qz, channel_u_w, channel_v_w, out)
                 tensor_mix(k)
             if 2 <= j < 2 + C_TILES // 2:
                 exponentials(0, C_TILES // 2 + j - 2)
-            if 0 <= k < C_TILES:
-                coefficients(k)
             if j < C_TILES:
                 quantise_queries(n + QUANTISE_AHEAD)
             if 0 <= k - 1 < TENSOR_TILES:
@@ -373,10 +358,13 @@ def tile_dynamicptheadselection_pa_kernel(tc, qz, channel_u_w, channel_v_w, out)
                 vector_mix(k)
             if j < C_TILES:
                 fold_bank(n, 1)
-                exponentials(1, j)
             if 0 <= k + 1 < C_TILES:
                 invert_sums(k + 1)
+            if j < C_TILES:
+                exponentials(1, j)
             if 0 <= k < C_TILES - 1:
                 finish_vector_columns(k, vector_columns(k))
+            if 0 <= k + 1 < C_TILES:
+                coefficients(k + 1)
         for i in range(E_BANKS):
             finish_vector_columns(C_TILES - 1, slice(i * BANK, (i + 1) * BANK))

@@ -84,6 +84,14 @@ def tile_dynamicptheadselection_pa_kernel(tc, qz, channel_u_w, channel_v_w, out)
         table_warmer = keep.tile([P, 1], F32, name="table_warmer")
         nc.scalar.activation(out=table_warmer[:], in_=identity[:, 0:1], func=EXP)
 
+        zeros = keep.tile([P, BANK], BF16, name="zeros")
+        nc.vector.memset(zeros[:], 0.0)
+
+        def keep_clock_up(count):
+            bank = work_bank([P, BANK], "unread")
+            for i in range(count):
+                nc.tensor.matmul(out=bank[:], lhsT=zeros[:, 0:P], rhs=zeros[:], start=True, stop=True)
+
         def copy_out(on_vector, out, in_):
             if on_vector:
                 nc.vector.tensor_copy(out=out, in_=in_)
@@ -118,30 +126,32 @@ def tile_dynamicptheadselection_pa_kernel(tc, qz, channel_u_w, channel_v_w, out)
         def transpose_x(j, on_vector):
             transpose_row_tile(x_rows[:, j, :], x_grouped[:], j * P, on_vector)
 
-        def quantise_x_pair(pair):
-            channels = slice(2 * pair * P, 2 * (pair + 1) * P)
-            values = slice(2 * pair * P * PACK, 2 * (pair + 1) * P * PACK)
+        def quantise_x(j, count):
+            channels = slice(j * P, (j + count) * P)
+            values = slice(j * P * PACK, (j + count) * P * PACK)
             for g in range(D_PASSES):
                 quantise(x_grouped[:, g, values], x_codes[:, g, channels], x_scales[:, g, channels])
 
-        def transpose_weights(w, h, vector_tiles, between=None):
-            w_grouped[w, h] = staging.tile(
-                [P, D_PASSES, R * PACK], BF16, tag="w_grouped", name="w_grouped", align_bytes=64
-            )
-            for t in range(PACK):
-                if between is not None and t == PACK - 1:
-                    between()
-                transpose_row_tile(w_rows[w, h][:, t, :], w_grouped[w, h][:], t * P, t in vector_tiles)
+        for h in range(HEADS):
+            for w in ("v", "u"):
+                w_codes[w, h] = keep.tile([P, D_PASSES, R], U32, name="%s%d_codes" % (w, h), align_bytes=64)
+                w_scales[w, h] = keep.tile([P, D_PASSES, R], U8, name="%s%d_scales" % (w, h), align_bytes=64)
+                q_codes[w, h] = keep.tile([P, C], U32, name="q%s%d_codes" % (w, h), align_bytes=64)
+                q_scales[w, h] = keep.tile([P, C], U8, name="q%s%d_scales" % (w, h), align_bytes=64)
+            q_grouped["v", h] = keep.tile([P, C, PACK], BF16, name="qv%d_grouped" % h, align_bytes=64)
 
-        def quantise_weights(w, h):
-            w_codes[w, h] = keep.tile([P, D_PASSES, R], U32, name="%s%d_codes" % (w, h), align_bytes=64)
-            w_scales[w, h] = keep.tile([P, D_PASSES, R], U8, name="%s%d_scales" % (w, h), align_bytes=64)
+        def transpose_weight_tile(w, h, t, on_vector):
+            if t == 0:
+                w_grouped[w, h] = staging.tile(
+                    [P, D_PASSES, R * PACK], BF16, tag="w_grouped", name="w_grouped", align_bytes=64
+                )
+            transpose_row_tile(w_rows[w, h][:, t, :], w_grouped[w, h][:], t * P, on_vector)
+
+        def quantise_weights(w, h, t=0, count=PACK):
+            columns = slice(t * P, (t + count) * P)
+            values = slice(t * P * PACK, (t + count) * P * PACK)
             for g in range(D_PASSES):
-                quantise(w_grouped[w, h][:, g, :], w_codes[w, h][:, g, :], w_scales[w, h][:, g, :])
-            if w == "v":
-                q_grouped[w, h] = keep.tile([P, C, PACK], BF16, name="q%s%d_grouped" % (w, h), align_bytes=64)
-            q_codes[w, h] = keep.tile([P, C], U32, name="q%s%d_codes" % (w, h), align_bytes=64)
-            q_scales[w, h] = keep.tile([P, C], U8, name="q%s%d_scales" % (w, h), align_bytes=64)
+                quantise(w_grouped[w, h][:, g, values], w_codes[w, h][:, g, columns], w_scales[w, h][:, g, columns])
 
         def project(w, h, j, target, on_vector):
             channels = slice(j * P, (j + 1) * P)
@@ -290,29 +300,53 @@ def tile_dynamicptheadselection_pa_kernel(tc, qz, channel_u_w, channel_v_w, out)
         def finish_vector_columns(j, keys):
             finish_columns(j, keys, exps(1, j)[:, keys])
 
-        transpose_weights("v", 0, (1,))
+        keep_clock_up(6)
+        transpose_weight_tile("v", 0, 0, False)
+        transpose_weight_tile("v", 0, 1, True)
+        keep_clock_up(1)
+        transpose_weight_tile("v", 0, 2, False)
+        quantise_weights("v", 0, 0, 2)
+        transpose_weight_tile("v", 0, 3, True)
+        keep_clock_up(1)
         transpose_x(0, False)
         transpose_x(1, False)
-        quantise_weights("v", 0)
+        keep_clock_up(1)
+        quantise_weights("v", 0, 2, 2)
         transpose_x(2, False)
+        quantise_x(0, 1)
         transpose_x(3, False)
-        quantise_x_pair(0)
+        quantise_x(1, 1)
+        project_keys(0, 0)
         transpose_x(4, True)
-        transpose_x(5, True)
-        quantise_x_pair(1)
-        for j in range(4):
-            project_keys(0, j, j == 2)
-        quantise_x_pair(2)
+        project_keys(0, 1)
+        quantise_x(2, 1)
+        quantise_x(3, 1)
+        transpose_x(5, False)
         transpose_x(6, True)
+        project_keys(0, 2, True)
         transpose_x(7, False)
-        transpose_weights("u", 0, (0, 2))
+        transpose_weight_tile("u", 0, 0, True)
+        quantise_x(4, 2)
+        transpose_weight_tile("u", 0, 1, False)
+        project_keys(0, 3)
+        transpose_weight_tile("u", 0, 2, True)
+        transpose_weight_tile("u", 0, 3, False)
+        quantise_x(6, 2)
+        transpose_weight_tile("u", 1, 0, False)
         quantise_keys(0, 0)
-        quantise_x_pair(3)
-        transpose_weights("u", 1, (3,), lambda: quantise_weights("u", 0))
-        transpose_weights("v", 1, (1, 3))
+        project_keys(0, 4)
+        transpose_weight_tile("u", 1, 1, False)
+        transpose_weight_tile("u", 1, 2, False)
+        quantise_weights("u", 0)
+        transpose_weight_tile("u", 1, 3, True)
+        project_keys(0, 5)
+        transpose_weight_tile("v", 1, 0, False)
+        transpose_weight_tile("v", 1, 1, True)
         quantise_weights("u", 1)
-        for j in range(4, 8):
-            project_keys(0, j)
+        transpose_weight_tile("v", 1, 2, False)
+        transpose_weight_tile("v", 1, 3, True)
+        project_keys(0, 6)
+        project_keys(0, 7)
         project_queries(0)
         project_queries(1)
         quantise_weights("v", 1)

@@ -28,8 +28,7 @@ QUERY_TILES = HEADS * C_TILES
 PROJECT_AHEAD = 3
 QUANTISE_AHEAD = 2
 LAG = 2
-TENSOR_FROM = BANK
-TENSOR_TILES = C_TILES - 1
+TENSOR_FROM = 576
 
 FLOPS = 2 * C * D * (2 * D) + HEADS * 2 * C * C * R
 
@@ -246,11 +245,9 @@ def tile_dynamicptheadselection_pa_kernel(tc, qz, channel_u_w, channel_v_w, out)
         inverse = keep.tile([P, C_TILES, HEADS], F32, name="inverse")
         coefficient = keep.tile([P, C_TILES, HEADS], F32, name="coefficient")
         tensor_columns = slice(TENSOR_FROM, C)
+        vector_columns = slice(0, TENSOR_FROM)
         mixed_bank = {}
         diagonal = {}
-
-        def vector_columns(j):
-            return slice(0, TENSOR_FROM if j < TENSOR_TILES else C)
 
         def invert_sums(j):
             nc.vector.reciprocal(out=inverse[:, j, :], in_=sums[:, j, 0:HEADS])
@@ -282,23 +279,21 @@ def tile_dynamicptheadselection_pa_kernel(tc, qz, channel_u_w, channel_v_w, out)
             nc.vector.tensor_tensor(
                 out=coefficient[:, j, :], in0=inverse[:, j, :], in1=sums[:, j, 1 : HEADS + 1], op=ALU.mult
             )
-            if j < TENSOR_TILES:
-                diagonal[j] = diagonals.tile([P, P], F32, tag="diagonal", name="diagonal")
-                nc.scalar.activation(out=diagonal[j][:], in_=identity[:], func=COPY, scale=coefficient[:, j, 0:1])
+            diagonal[j] = diagonals.tile([P, P], F32, tag="diagonal", name="diagonal")
+            nc.scalar.activation(out=diagonal[j][:], in_=identity[:], func=COPY, scale=coefficient[:, j, 0:1])
 
         def vector_mix(j):
-            keys = vector_columns(j)
             nc.vector.scalar_tensor_tensor(
-                out=exps(1, j)[:, keys],
-                in0=exps(0, j)[:, keys],
+                out=exps(1, j)[:, vector_columns],
+                in0=exps(0, j)[:, vector_columns],
                 scalar=coefficient[:, j, 0:1],
-                in1=exps(1, j)[:, keys],
+                in1=exps(1, j)[:, vector_columns],
                 op0=ALU.mult,
                 op1=ALU.add,
             )
 
-        def finish_vector_columns(j, keys):
-            finish_columns(j, keys, exps(1, j)[:, keys])
+        def finish_vector_columns(j):
+            finish_columns(j, vector_columns, exps(1, j)[:, vector_columns])
 
         keep_clock_up(6)
         transpose_weight_tile("v", 0, 0, False)
@@ -380,13 +375,13 @@ def tile_dynamicptheadselection_pa_kernel(tc, qz, channel_u_w, channel_v_w, out)
                 fold_bank(n, 0)
                 project_queries(n + PROJECT_AHEAD)
                 logit_banks(n + 1)
-            if 0 <= k < TENSOR_TILES:
+            if 0 <= k < C_TILES:
                 tensor_mix(k)
             if 2 <= j < 2 + C_TILES // 2:
                 exponentials(0, C_TILES // 2 + j - 2)
             if j < C_TILES:
                 quantise_queries(n + QUANTISE_AHEAD)
-            if 0 <= k - 1 < TENSOR_TILES:
+            if 0 <= k - 1 < C_TILES:
                 finish_tensor_columns(k - 1)
             if 0 <= k < C_TILES:
                 vector_mix(k)
@@ -396,9 +391,7 @@ def tile_dynamicptheadselection_pa_kernel(tc, qz, channel_u_w, channel_v_w, out)
                 invert_sums(k + 1)
             if j < C_TILES:
                 exponentials(1, j)
-            if 0 <= k < C_TILES - 1:
-                finish_vector_columns(k, vector_columns(k))
+            if 0 <= k < C_TILES:
+                finish_vector_columns(k)
             if 0 <= k + 1 < C_TILES:
                 coefficients(k + 1)
-        for i in range(E_BANKS):
-            finish_vector_columns(C_TILES - 1, slice(i * BANK, (i + 1) * BANK))

@@ -295,7 +295,7 @@ def tile_dynamicptheadselection_pa_kernel(tc, qz, channel_u_w, channel_v_w, out)
         def finish_vector_columns(j):
             finish_columns(j, vector_columns, exps(1, j)[:, vector_columns])
 
-        keep_clock_up(6)
+        keep_clock_up(3)
         transpose_weight_tile("v", 0, 0, False)
         transpose_weight_tile("v", 0, 1, True)
         keep_clock_up(1)

@@ -75,8 +75,8 @@ def tile_dynamicptheadselection_pa_kernel(tc, qz, channel_u_w, channel_v_w, out)
         for j in range(C_TILES):
             nc.sync.dma_start(out=x_rows[:, j, :], in_=x_dram[:, j, :])
         load_weights("u", 0, 2)
-        load_weights("u", 1, 2)
         load_weights("v", 1, 2)
+        load_weights("u", 1, 2)
 
         identity = keep.tile([P, P], F32, name="identity")
         make_identity(nc, identity[:])
@@ -298,54 +298,43 @@ def tile_dynamicptheadselection_pa_kernel(tc, qz, channel_u_w, channel_v_w, out)
         keep_clock_up(3)
         transpose_weight_tile("v", 0, 0, False)
         transpose_weight_tile("v", 0, 1, True)
-        keep_clock_up(1)
-        transpose_weight_tile("v", 0, 2, False)
         quantise_weights("v", 0, 0, 2)
+        transpose_weight_tile("v", 0, 2, False)
         transpose_weight_tile("v", 0, 3, True)
-        keep_clock_up(1)
         transpose_x(0, False)
         transpose_x(1, False)
-        keep_clock_up(1)
         quantise_weights("v", 0, 2, 2)
         transpose_x(2, False)
         quantise_x(0, 1)
         transpose_x(3, False)
         quantise_x(1, 1)
-        project_keys(0, 0)
         transpose_x(4, True)
+        project_keys(0, 0)
         project_keys(0, 1)
-        quantise_x(2, 1)
-        quantise_x(3, 1)
+        quantise_x(2, 2)
         transpose_x(5, False)
         transpose_x(6, True)
-        project_keys(0, 2, True)
         transpose_x(7, False)
-        transpose_weight_tile("u", 0, 0, True)
-        quantise_x(4, 2)
-        transpose_weight_tile("u", 0, 1, False)
+        project_keys(0, 2, True)
         project_keys(0, 3)
-        transpose_weight_tile("u", 0, 2, True)
-        transpose_weight_tile("u", 0, 3, False)
-        quantise_x(6, 2)
-        transpose_weight_tile("u", 1, 0, False)
+        quantise_x(4, 2)
+        for t in range(PACK):
+            transpose_weight_tile("u", 0, t, t % 2 == 0)
         quantise_keys(0, 0)
-        project_keys(0, 4)
-        transpose_weight_tile("u", 1, 1, False)
-        transpose_weight_tile("u", 1, 2, False)
+        quantise_x(6, 2)
+        for j in range(4, C_TILES):
+            project_keys(0, j)
         quantise_weights("u", 0)
+        for t in range(PACK):
+            transpose_weight_tile("v", 1, t, t % 2 == 1)
+        transpose_weight_tile("u", 1, 0, False)
+        transpose_weight_tile("u", 1, 1, False)
+        quantise_keys(0, 1)
+        quantise_weights("v", 1)
+        transpose_weight_tile("u", 1, 2, False)
         transpose_weight_tile("u", 1, 3, True)
-        project_keys(0, 5)
-        transpose_weight_tile("v", 1, 0, False)
-        transpose_weight_tile("v", 1, 1, True)
-        quantise_weights("u", 1)
-        transpose_weight_tile("v", 1, 2, False)
-        transpose_weight_tile("v", 1, 3, True)
-        project_keys(0, 6)
-        project_keys(0, 7)
         project_queries(0)
         project_queries(1)
-        quantise_weights("v", 1)
-        quantise_keys(0, 1)
         quantise_queries(0)
         project_queries(2)
         quantise_queries(1)
@@ -354,6 +343,8 @@ def tile_dynamicptheadselection_pa_kernel(tc, qz, channel_u_w, channel_v_w, out)
         logit_banks(0)
 
         for n in range(C_TILES):
+            if n == 2:
+                quantise_weights("u", 1)
             fold_bank(n, 0)
             project_queries(n + PROJECT_AHEAD)
             if n + 1 < C_TILES:

@@ -28,7 +28,8 @@ QUERY_TILES = HEADS * C_TILES
 PROJECT_AHEAD = 3
 QUANTISE_AHEAD = 2
 LAG = 2
-TENSOR_FROM = 576
+LAST_FOLDS = 6
+TENSOR_FROM = 512
 
 FLOPS = 2 * C * D * (2 * D) + HEADS * 2 * C * C * R
 
@@ -47,7 +48,7 @@ def tile_dynamicptheadselection_pa_kernel(tc, qz, channel_u_w, channel_v_w, out)
         ctx.enter_context(tc.manual_schedule())
         keep = ctx.enter_context(tc.tile_pool(name="keep", bufs=1))
         staging = ctx.enter_context(tc.tile_pool(name="staging", bufs=3))
-        results = ctx.enter_context(tc.tile_pool(name="results", bufs=LAG + 4))
+        results = ctx.enter_context(tc.tile_pool(name="results", bufs=C_TILES))
         queries = ctx.enter_context(tc.tile_pool(name="queries", bufs=4))
         diagonals = ctx.enter_context(tc.tile_pool(name="diagonals", bufs=4))
         logit_pool = ctx.enter_context(tc.psum_pool(name="logit_pool", bufs=4))
@@ -306,10 +307,10 @@ def tile_dynamicptheadselection_pa_kernel(tc, qz, channel_u_w, channel_v_w, out)
         quantise_weights("v", 0, 2, 2)
         transpose_x(2, False)
         quantise_x(0, 1)
+        project_keys(0, 0)
         transpose_x(3, False)
         quantise_x(1, 1)
         transpose_x(4, True)
-        project_keys(0, 0)
         project_keys(0, 1)
         quantise_x(2, 2)
         transpose_x(5, False)
@@ -366,13 +367,16 @@ def tile_dynamicptheadselection_pa_kernel(tc, qz, channel_u_w, channel_v_w, out)
                 fold_bank(n, 0)
                 project_queries(n + PROJECT_AHEAD)
                 logit_banks(n + 1)
+            if j == C_TILES:
+                for q in range(LAST_FOLDS - LAG - 1, k - 1):
+                    finish_tensor_columns(q)
             if 0 <= k < C_TILES:
                 tensor_mix(k)
             if 2 <= j < 2 + C_TILES // 2:
                 exponentials(0, C_TILES // 2 + j - 2)
             if j < C_TILES:
                 quantise_queries(n + QUANTISE_AHEAD)
-            if 0 <= k - 1 < C_TILES:
+            if 0 <= k - 1 < C_TILES and not LAST_FOLDS <= j < C_TILES:
                 finish_tensor_columns(k - 1)
             if 0 <= k < C_TILES:
                 vector_mix(k)

@@ -29,7 +29,7 @@ PROJECT_AHEAD = 3
 QUANTISE_AHEAD = 2
 LAG = 2
 LAST_FOLDS = 6
-TENSOR_FROM = 512
+TENSOR_FROM = 576
 
 FLOPS = 2 * C * D * (2 * D) + HEADS * 2 * C * C * R
 
@@ -37,8 +37,8 @@ FLOPS = 2 * C * D * (2 * D) + HEADS * 2 * C * C * R
 def tile_dynamicptheadselection_pa_kernel(tc, qz, channel_u_w, channel_v_w, out):
     nc = tc.nc
 
-    x_dram = qz.flatten_outer_dims().rearrange("(j p) d -> p j d", p=P)
-    out_dram = out.flatten_outer_dims().rearrange("(j p) e -> p j e", p=P)
+    x_dram = qz.flatten_outer_dims().rearrange("(p j) d -> p j d", p=P)
+    out_dram = out.flatten_outer_dims().rearrange("(p j) e -> p j e", p=P)
     w_dram = {
         "u": channel_u_w.flatten_outer_dims().rearrange("(h p t) d -> h p t d", h=HEADS, t=PACK),
         "v": channel_v_w.flatten_outer_dims().rearrange("(h p t) d -> h p t d", h=HEADS, t=PACK),
@@ -73,8 +73,8 @@ def tile_dynamicptheadselection_pa_kernel(tc, qz, channel_u_w, channel_v_w, out)
                 nc.sync.dma_start(out=w_rows[w, h][:, t : t + count, :], in_=w_dram[w][h, :, t : t + count, :])
 
         load_weights("v", 0, 1)
-        for j in range(C_TILES):
-            nc.sync.dma_start(out=x_rows[:, j, :], in_=x_dram[:, j, :])
+        for j in range(0, C_TILES, 2):
+            nc.sync.dma_start(out=x_rows[:, j : j + 2, :], in_=x_dram[:, j : j + 2, :])
         load_weights("u", 0, 2)
         load_weights("v", 1, 2)
         load_weights("u", 1, 2)
@@ -223,9 +223,10 @@ def tile_dynamicptheadselection_pa_kernel(tc, qz, channel_u_w, channel_v_w, out)
             h, j = divmod(n, C_TILES)
             if h == 1 and i == 0:
                 exp_head1[j] = results.tile([P, C], F32, tag="exp_head1", name="exp_head1")
+            row_tiles = slice(i * BANK // P, (i + 1) * BANK // P)
             nc.vector.tensor_scalar(
-                out=exps(h, j)[:, i * BANK : (i + 1) * BANK],
-                in0=filled[n, i][:],
+                out=exps(h, j).rearrange("p (q m) -> p q m", m=C_TILES)[:, :, row_tiles],
+                in0=filled[n, i][:].rearrange("p (m q) -> p q m", q=P),
                 scalar1=-1.0 / math.sqrt(R),
                 scalar2=(None if i == 0 else lowest[:, h, j, i - 1 : i]),
                 op0=ALU.mult,
@@ -307,10 +308,10 @@ def tile_dynamicptheadselection_pa_kernel(tc, qz, channel_u_w, channel_v_w, out)
         quantise_weights("v", 0, 2, 2)
         transpose_x(2, False)
         quantise_x(0, 1)
-        project_keys(0, 0)
         transpose_x(3, False)
         quantise_x(1, 1)
         transpose_x(4, True)
+        project_keys(0, 0)
         project_keys(0, 1)
         quantise_x(2, 2)
         transpose_x(5, False)

@@ -278,7 +278,7 @@ def tile_dynamicptheadselection_pa_kernel(tc, qz, channel_u_w, channel_v_w, out)
             finish_columns(j, tensor_columns, mixed_bank[j][:])
 
         def coefficients(j):
-            nc.vector.tensor_tensor(
+            nc.gpsimd.tensor_tensor(
                 out=coefficient[:, j, :], in0=inverse[:, j, :], in1=sums[:, j, 1 : HEADS + 1], op=ALU.mult
             )
             diagonal[j] = diagonals.tile([P, P], F32, tag="diagonal", name="diagonal")

@@ -11,7 +11,6 @@ U8 = mybir.dt.uint8
 FP8X4 = mybir.dt.float8_e4m3fn_x4
 ALU = mybir.AluOpType
 EXP = mybir.ActivationFunctionType.Exp
-COPY = mybir.ActivationFunctionType.Copy
 
 P = 128
 PACK = 4
@@ -177,8 +176,9 @@ def tile_dynamicptheadselection_pa_kernel(tc, qz, channel_u_w, channel_v_w, out)
         def project_keys(h, j, on_vector=False):
             project("v", h, j, q_grouped["v", h][:, j * P : (j + 1) * P, :], on_vector)
 
-        def quantise_keys(h, i):
-            quantise_projection("v", h, q_grouped["v", h][:, i * BANK : (i + 1) * BANK, :], i * BANK, BANK)
+        def quantise_keys(h, first, count=BANK):
+            keys = slice(first, first + count)
+            quantise_projection("v", h, q_grouped["v", h][:, keys, :], first, count)
 
         def project_queries(n):
             if n < QUERY_TILES:
@@ -282,7 +282,14 @@ def tile_dynamicptheadselection_pa_kernel(tc, qz, channel_u_w, channel_v_w, out)
                 out=coefficient[:, j, :], in0=inverse[:, j, :], in1=sums[:, j, 1 : HEADS + 1], op=ALU.mult
             )
             diagonal[j] = diagonals.tile([P, P], F32, tag="diagonal", name="diagonal")
-            nc.scalar.activation(out=diagonal[j][:], in_=identity[:], func=COPY, scale=coefficient[:, j, 0:1])
+            nc.gpsimd.tensor_scalar(
+                out=diagonal[j][:],
+                in0=identity[:],
+                scalar1=coefficient[:, j, 0:1],
+                scalar2=0.0,
+                op0=ALU.mult,
+                op1=ALU.add,
+            )
 
         def vector_mix(j):
             nc.vector.scalar_tensor_tensor(
@@ -331,7 +338,7 @@ def tile_dynamicptheadselection_pa_kernel(tc, qz, channel_u_w, channel_v_w, out)
             transpose_weight_tile("v", 1, t, t % 2 == 1)
         transpose_weight_tile("u", 1, 0, False)
         transpose_weight_tile("u", 1, 1, False)
-        quantise_keys(0, 1)
+        quantise_keys(0, BANK)
         quantise_weights("v", 1)
         transpose_weight_tile("u", 1, 2, False)
         transpose_weight_tile("u", 1, 3, True)
@@ -354,8 +361,8 @@ def tile_dynamicptheadselection_pa_kernel(tc, qz, channel_u_w, channel_v_w, out)
             quantise_queries(n + QUANTISE_AHEAD)
             if n == C_TILES // 2:
                 quantise_keys(1, 0)
-            if n == C_TILES - 1:
-                quantise_keys(1, 1)
+            if n >= C_TILES - 2:
+                quantise_keys(1, BANK + (n - (C_TILES - 2)) * BANK // 2, BANK // 2)
             logit_banks(n + 1)
             fold_bank(n, 1)
             if n % 2 == 1:
@@ -385,9 +392,8 @@ def tile_dynamicptheadselection_pa_kernel(tc, qz, channel_u_w, channel_v_w, out)
                 fold_bank(n, 1)
             if 0 <= k + 1 < C_TILES:
                 invert_sums(k + 1)
+                coefficients(k + 1)
             if j < C_TILES:
                 exponentials(1, j)
             if 0 <= k < C_TILES:
                 finish_vector_columns(k)
-            if 0 <= k + 1 < C_TILES:
-                coefficients(k + 1)

@@ -327,10 +327,12 @@ def tile_dynamicptheadselection_pa_kernel(tc, qz, channel_u_w, channel_v_w, out)
         project_keys(0, 2, True)
         project_keys(0, 3)
         quantise_x(4, 2)
-        for t in range(PACK):
-            transpose_weight_tile("u", 0, t, t % 2 == 0)
+        transpose_weight_tile("u", 0, 0, True)
+        transpose_weight_tile("u", 0, 1, False)
         quantise_keys(0, 0)
         quantise_x(6, 2)
+        transpose_weight_tile("u", 0, 2, True)
+        transpose_weight_tile("u", 0, 3, False)
         for j in range(4, C_TILES):
             project_keys(0, j)
         quantise_weights("u", 0)
@@ -368,32 +370,36 @@ def tile_dynamicptheadselection_pa_kernel(tc, qz, channel_u_w, channel_v_w, out)
             if n % 2 == 1:
                 exponentials(0, n // 2)
 
-        for j in range(C_TILES + LAG + 1):
+        for j in range(C_TILES):
             n = C_TILES + j
             k = j - LAG
-            if j < C_TILES:
-                fold_bank(n, 0)
-                project_queries(n + PROJECT_AHEAD)
-                logit_banks(n + 1)
-            if j == C_TILES:
-                for q in range(LAST_FOLDS - LAG - 1, k - 1):
-                    finish_tensor_columns(q)
-            if 0 <= k < C_TILES:
+            fold_bank(n, 0)
+            project_queries(n + PROJECT_AHEAD)
+            logit_banks(n + 1)
+            if k >= 0:
                 tensor_mix(k)
             if 2 <= j < 2 + C_TILES // 2:
                 exponentials(0, C_TILES // 2 + j - 2)
-            if j < C_TILES:
-                quantise_queries(n + QUANTISE_AHEAD)
-            if 0 <= k - 1 < C_TILES and not LAST_FOLDS <= j < C_TILES:
+            quantise_queries(n + QUANTISE_AHEAD)
+            if k >= 1 and j < LAST_FOLDS:
                 finish_tensor_columns(k - 1)
-            if 0 <= k < C_TILES:
+            if k >= 0:
                 vector_mix(k)
-            if j < C_TILES:
-                fold_bank(n, 1)
-            if 0 <= k + 1 < C_TILES:
+            fold_bank(n, 1)
+            if k >= -1:
                 invert_sums(k + 1)
                 coefficients(k + 1)
-            if j < C_TILES:
-                exponentials(1, j)
-            if 0 <= k < C_TILES:
+            exponentials(1, j)
+            if k >= 0:
                 finish_vector_columns(k)
+
+        for k in range(LAST_FOLDS - LAG - 1, C_TILES - LAG - 1):
+            finish_tensor_columns(k)
+        invert_sums(C_TILES - 1)
+        coefficients(C_TILES - 1)
+        for k in range(C_TILES - LAG, C_TILES):
+            tensor_mix(k)
+            vector_mix(k)
+            finish_tensor_columns(k - 1)
+            finish_vector_columns(k)
+        finish_tensor_columns(C_TILES - 1)

import math
from contextlib import ExitStack

import concourse.mybir as mybir
from concourse.masks import make_identity

F32 = mybir.dt.float32
BF16 = mybir.dt.bfloat16
U32 = mybir.dt.uint32
U8 = mybir.dt.uint8
FP8X4 = mybir.dt.float8_e4m3fn_x4
ALU = mybir.AluOpType
EXP = mybir.ActivationFunctionType.Exp

P = 128
PACK = 4
K_PASS = P * PACK
C = 1024
D = 1024
HEADS = 2
R = D // HEADS
C_TILES = C // P
D_PASSES = D // K_PASS
BANK = 512
E_BANKS = C // BANK
QUERY_TILES = HEADS * C_TILES
PROJECT_AHEAD = 3
QUANTISE_AHEAD = 2
LAG = 2
LAST_FOLDS = 6
TENSOR_FROM = 576

FLOPS = 2 * C * D * (2 * D) + HEADS * 2 * C * C * R


def tile_dynamicptheadselection_pa_kernel(tc, qz, channel_u_w, channel_v_w, out):
    nc = tc.nc

    x_dram = qz.flatten_outer_dims().rearrange("(p j) d -> p j d", p=P)
    out_dram = out.flatten_outer_dims().rearrange("(p j) e -> p j e", p=P)
    w_dram = {
        "u": channel_u_w.flatten_outer_dims().rearrange("(h p t) d -> h p t d", h=HEADS, t=PACK),
        "v": channel_v_w.flatten_outer_dims().rearrange("(h p t) d -> h p t d", h=HEADS, t=PACK),
    }

    with ExitStack() as ctx:
        ctx.enter_context(tc.manual_schedule())
        keep = ctx.enter_context(tc.tile_pool(name="keep", bufs=1))
        staging = ctx.enter_context(tc.tile_pool(name="staging", bufs=3))
        results = ctx.enter_context(tc.tile_pool(name="results", bufs=C_TILES))
        queries = ctx.enter_context(tc.tile_pool(name="queries", bufs=4))
        diagonals = ctx.enter_context(tc.tile_pool(name="diagonals", bufs=4))
        logit_pool = ctx.enter_context(tc.psum_pool(name="logit_pool", bufs=4))
        work_pool = ctx.enter_context(tc.psum_pool(name="work_pool", bufs=4))
        spare_logit_banks = [True, True]

        def work_bank(shape, name):
            use_logit_bank = spare_logit_banks[0] and spare_logit_banks[1]
            spare_logit_banks[1] = not spare_logit_banks[1]
            if use_logit_bank:
                return logit_pool.tile(shape, F32, tag="logits", name=name)
            return work_pool.tile(shape, F32, tag="work", name=name)

        x_rows = keep.tile([P, C_TILES, D], BF16, name="x_rows")
        w_rows = {}
        for h in range(HEADS):
            for w in ("v", "u"):
                w_rows[w, h] = keep.tile([P, PACK, D], BF16, name="%s%d_rows" % (w, h))

        def load_weights(w, h, count):
            for t in range(0, PACK, count):
                nc.sync.dma_start(out=w_rows[w, h][:, t : t + count, :], in_=w_dram[w][h, :, t : t + count, :])

        load_weights("v", 0, 1)
        for j in range(0, C_TILES, 2):
            nc.sync.dma_start(out=x_rows[:, j : j + 2, :], in_=x_dram[:, j : j + 2, :])
        load_weights("u", 0, 2)
        load_weights("v", 1, 2)
        load_weights("u", 1, 2)

        identity = keep.tile([P, P], F32, name="identity")
        make_identity(nc, identity[:])
        table_warmer = keep.tile([P, 1], F32, name="table_warmer")
        nc.scalar.activation(out=table_warmer[:], in_=identity[:, 0:1], func=EXP)

        zeros = keep.tile([P, BANK], BF16, name="zeros")
        nc.vector.memset(zeros[:], 0.0)

        def keep_clock_up(count):
            bank = work_bank([P, BANK], "unread")
            for i in range(count):
                nc.tensor.matmul(out=bank[:], lhsT=zeros[:, 0:P], rhs=zeros[:], start=True, stop=True)

        def copy_out(on_vector, out, in_):
            if on_vector:
                nc.vector.tensor_copy(out=out, in_=in_)
            else:
                nc.scalar.copy(out=out, in_=in_)

        def quantise(grouped, codes, scales):
            nc.vector.quantize_mx(out=codes.bitcast(FP8X4), scales=scales, in_=grouped)

        def transpose_row_tile(rows, grouped, first_column, on_vector):
            words = rows.bitcast(F32)
            bank = work_bank([P, 2 * D_PASSES, P], "transposed")
            for k in range(2 * D_PASSES):
                nc.tensor.transpose(bank[:, k, :], words[:, k * P : (k + 1) * P], identity[:])
            grouped_words = grouped.bitcast(F32).rearrange("p g (c u) -> p g c u", u=2)
            copy_out(
                on_vector,
                grouped_words[:, :, first_column : first_column + P, :],
                bank[:].rearrange("p (g u) c -> p g c u", u=2),
            )

        x_grouped = keep.tile([P, D_PASSES, C * PACK], BF16, name="x_grouped", align_bytes=64)
        x_codes = keep.tile([P, D_PASSES, C], U32, name="x_codes", align_bytes=64)
        x_scales = keep.tile([P, D_PASSES, C], U8, name="x_scales", align_bytes=64)
        w_grouped = {}
        w_codes = {}
        w_scales = {}
        q_grouped = {}
        q_codes = {}
        q_scales = {}

        def transpose_x(j, on_vector):
            transpose_row_tile(x_rows[:, j, :], x_grouped[:], j * P, on_vector)

        def quantise_x(j, count):
            channels = slice(j * P, (j + count) * P)
            values = slice(j * P * PACK, (j + count) * P * PACK)
            for g in range(D_PASSES):
                quantise(x_grouped[:, g, values], x_codes[:, g, channels], x_scales[:, g, channels])

        for h in range(HEADS):
            for w in ("v", "u"):
                w_codes[w, h] = keep.tile([P, D_PASSES, R], U32, name="%s%d_codes" % (w, h), align_bytes=64)
                w_scales[w, h] = keep.tile([P, D_PASSES, R], U8, name="%s%d_scales" % (w, h), align_bytes=64)
                q_codes[w, h] = keep.tile([P, C], U32, name="q%s%d_codes" % (w, h), align_bytes=64)
                q_scales[w, h] = keep.tile([P, C], U8, name="q%s%d_scales" % (w, h), align_bytes=64)
            q_grouped["v", h] = keep.tile([P, C, PACK], BF16, name="qv%d_grouped" % h, align_bytes=64)

        def transpose_weight_tile(w, h, t, on_vector):
            if t == 0:
                w_grouped[w, h] = staging.tile(
                    [P, D_PASSES, R * PACK], BF16, tag="w_grouped", name="w_grouped", align_bytes=64
                )
            transpose_row_tile(w_rows[w, h][:, t, :], w_grouped[w, h][:], t * P, on_vector)

        def quantise_weights(w, h, t=0, count=PACK):
            columns = slice(t * P, (t + count) * P)
            values = slice(t * P * PACK, (t + count) * P * PACK)
            for g in range(D_PASSES):
                quantise(w_grouped[w, h][:, g, values], w_codes[w, h][:, g, columns], w_scales[w, h][:, g, columns])

        def project(w, h, j, target, on_vector):
            channels = slice(j * P, (j + 1) * P)
            bank = work_bank([P, PACK, P], "projected")
            for t in range(PACK):
                rows_t = slice(t * P, (t + 1) * P)
                for g in range(D_PASSES):
                    nc.tensor.matmul_mx(
                        out=bank[:, t, :],
                        lhsT=w_codes[w, h][:, g, rows_t].bitcast(FP8X4),
                        lhsT_scale=w_scales[w, h][:, g, rows_t],
                        rhs=x_codes[:, g, channels].bitcast(FP8X4),
                        rhs_scale=x_scales[:, g, channels],
                        start=(g == 0),
                        stop=(g == D_PASSES - 1),
                    )
            copy_out(on_vector, target, bank[:].rearrange("p t c -> p c t"))

        def quantise_projection(w, h, grouped, first, count):
            channels = slice(first, first + count)
            quantise(grouped.rearrange("p c t -> p (c t)"), q_codes[w, h][:, channels], q_scales[w, h][:, channels])

        def project_keys(h, j, on_vector=False):
            project("v", h, j, q_grouped["v", h][:, j * P : (j + 1) * P, :], on_vector)

        def quantise_keys(h, first, count=BANK):
            keys = slice(first, first + count)
            quantise_projection("v", h, q_grouped["v", h][:, keys, :], first, count)

        def project_queries(n):
            if n < QUERY_TILES:
                h, j = divmod(n, C_TILES)
                q_grouped["u", h, j] = queries.tile([P, P, PACK], BF16, tag="queries", name="queries", align_bytes=64)
                project("u", h, j, q_grouped["u", h, j][:], False)

        def quantise_queries(n):
            if n < QUERY_TILES:
                h, j = divmod(n, C_TILES)
                quantise_projection("u", h, q_grouped["u", h, j][:], j * P, P)

        lowest = keep.tile([P, HEADS, C_TILES, E_BANKS], F32, name="lowest")
        sums = keep.tile([P, C_TILES, HEADS + 1], F32, name="sums")
        nc.vector.memset(sums[:], 0.5)
        exp_head0 = keep.tile([P, C_TILES, C], F32, name="exp_head0")
        exp_head1 = {}

        def exps(h, j):
            return exp_head0[:, j, :] if h == 0 else exp_head1[j][:]

        filled = {}

        def logit_banks(n):
            if n < QUERY_TILES:
                h, j = divmod(n, C_TILES)
                rows = slice(j * P, (j + 1) * P)
                for i in range(E_BANKS):
                    keys = slice(i * BANK, (i + 1) * BANK)
                    filled[n, i] = logit_pool.tile([P, BANK], F32, tag="logits", name="logit_bank")
                    nc.tensor.matmul_mx(
                        out=filled[n, i][:],
                        lhsT=q_codes["u", h][:, rows].bitcast(FP8X4),
                        lhsT_scale=q_scales["u", h][:, rows],
                        rhs=q_codes["v", h][:, keys].bitcast(FP8X4),
                        rhs_scale=q_scales["v", h][:, keys],
                        start=True,
                        stop=True,
                    )

        def fold_bank(n, i):
            h, j = divmod(n, C_TILES)
            if h == 1 and i == 0:
                exp_head1[j] = results.tile([P, C], F32, tag="exp_head1", name="exp_head1")
            row_tiles = slice(i * BANK // P, (i + 1) * BANK // P)
            nc.vector.tensor_scalar(
                out=exps(h, j).rearrange("p (q m) -> p q m", m=C_TILES)[:, :, row_tiles],
                in0=filled[n, i][:].rearrange("p (m q) -> p q m", q=P),
                scalar1=-1.0 / math.sqrt(R),
                scalar2=(None if i == 0 else lowest[:, h, j, i - 1 : i]),
                op0=ALU.mult,
                op1=ALU.min,
                accum_out=lowest[:, h, j, i : i + 1],
            )

        def exponentials(h, j):
            nc.scalar.activation(
                out=exps(h, j),
                in_=exps(h, j),
                func=EXP,
                bias=lowest[:, h, j, E_BANKS - 1 : E_BANKS],
                scale=-1.0,
                accum_out=sums[:, j, h : h + 1],
            )

        inverse = keep.tile([P, C_TILES, HEADS], F32, name="inverse")
        coefficient = keep.tile([P, C_TILES, HEADS], F32, name="coefficient")
        tensor_columns = slice(TENSOR_FROM, C)
        vector_columns = slice(0, TENSOR_FROM)
        mixed_bank = {}
        diagonal = {}

        def invert_sums(j):
            nc.vector.reciprocal(out=inverse[:, j, :], in_=sums[:, j, 0:HEADS])

        def tensor_mix(j):
            mixed_bank[j] = work_bank([P, C - TENSOR_FROM], "mixed")
            nc.tensor.matmul(
                out=mixed_bank[j][:], lhsT=identity[:], rhs=exps(1, j)[:, tensor_columns], start=True, stop=False
            )
            nc.tensor.matmul(
                out=mixed_bank[j][:], lhsT=diagonal[j][:], rhs=exps(0, j)[:, tensor_columns], start=False, stop=True
            )

        def finish_columns(j, keys, mixed):
            nc.vector.scalar_tensor_tensor(
                out=exps(1, j)[:, keys],
                in0=mixed,
                scalar=coefficient[:, j, 1:2],
                in1=x_rows[:, j, keys],
                op0=ALU.mult,
                op1=ALU.mult,
            )
            nc.sync.dma_start(out=out_dram[:, j, keys], in_=exps(1, j)[:, keys])

        def finish_tensor_columns(j):
            finish_columns(j, tensor_columns, mixed_bank[j][:])

        def coefficients(j):
            nc.gpsimd.tensor_tensor(
                out=coefficient[:, j, :], in0=inverse[:, j, :], in1=sums[:, j, 1 : HEADS + 1], op=ALU.mult
            )
            diagonal[j] = diagonals.tile([P, P], F32, tag="diagonal", name="diagonal")
            nc.gpsimd.tensor_scalar(
                out=diagonal[j][:],
                in0=identity[:],
                scalar1=coefficient[:, j, 0:1],
                scalar2=0.0,
                op0=ALU.mult,
                op1=ALU.add,
            )

        def vector_mix(j):
            nc.vector.scalar_tensor_tensor(
                out=exps(1, j)[:, vector_columns],
                in0=exps(0, j)[:, vector_columns],
                scalar=coefficient[:, j, 0:1],
                in1=exps(1, j)[:, vector_columns],
                op0=ALU.mult,
                op1=ALU.add,
            )

        def finish_vector_columns(j):
            finish_columns(j, vector_columns, exps(1, j)[:, vector_columns])

        keep_clock_up(3)
        transpose_weight_tile("v", 0, 0, False)
        transpose_weight_tile("v", 0, 1, True)
        quantise_weights("v", 0, 0, 2)
        transpose_weight_tile("v", 0, 2, False)
        transpose_weight_tile("v", 0, 3, True)
        transpose_x(0, False)
        transpose_x(1, False)
        quantise_weights("v", 0, 2, 2)
        transpose_x(2, False)
        quantise_x(0, 1)
        transpose_x(3, False)
        quantise_x(1, 1)
        transpose_x(4, True)
        project_keys(0, 0)
        project_keys(0, 1)
        quantise_x(2, 2)
        transpose_x(5, False)
        transpose_x(6, True)
        transpose_x(7, False)
        project_keys(0, 2, True)
        project_keys(0, 3)
        quantise_x(4, 2)
        transpose_weight_tile("u", 0, 0, True)
        transpose_weight_tile("u", 0, 1, False)
        quantise_keys(0, 0)
        quantise_x(6, 2)
        transpose_weight_tile("u", 0, 2, True)
        transpose_weight_tile("u", 0, 3, False)
        for j in range(4, C_TILES):
            project_keys(0, j)
        quantise_weights("u", 0)
        for t in range(PACK):
            transpose_weight_tile("v", 1, t, t % 2 == 1)
        transpose_weight_tile("u", 1, 0, False)
        transpose_weight_tile("u", 1, 1, False)
        quantise_keys(0, BANK)
        quantise_weights("v", 1)
        transpose_weight_tile("u", 1, 2, False)
        transpose_weight_tile("u", 1, 3, True)
        project_queries(0)
        project_queries(1)
        quantise_queries(0)
        project_queries(2)
        quantise_queries(1)
        spare_logit_banks[0] = False
        project_keys(1, 0)
        logit_banks(0)

        for n in range(C_TILES):
            if n == 2:
                quantise_weights("u", 1)
            fold_bank(n, 0)
            project_queries(n + PROJECT_AHEAD)
            if n + 1 < C_TILES:
                project_keys(1, n + 1)
            quantise_queries(n + QUANTISE_AHEAD)
            if n == C_TILES // 2:
                quantise_keys(1, 0)
            if n >= C_TILES - 2:
                quantise_keys(1, BANK + (n - (C_TILES - 2)) * BANK // 2, BANK // 2)
            logit_banks(n + 1)
            fold_bank(n, 1)
            if n % 2 == 1:
                exponentials(0, n // 2)

        for j in range(C_TILES):
            n = C_TILES + j
            k = j - LAG
            fold_bank(n, 0)
            project_queries(n + PROJECT_AHEAD)
            logit_banks(n + 1)
            if k >= 0:
                tensor_mix(k)
            if 2 <= j < 2 + C_TILES // 2:
                exponentials(0, C_TILES // 2 + j - 2)
            quantise_queries(n + QUANTISE_AHEAD)
            if k >= 1 and j < LAST_FOLDS:
                finish_tensor_columns(k - 1)
            if k >= 0:
                vector_mix(k)
            fold_bank(n, 1)
            if k >= -1:
                invert_sums(k + 1)
                coefficients(k + 1)
            exponentials(1, j)
            if k >= 0:
                finish_vector_columns(k)

        for k in range(LAST_FOLDS - LAG - 1, C_TILES - LAG - 1):
            finish_tensor_columns(k)
        invert_sums(C_TILES - 1)
        coefficients(C_TILES - 1)
        for k in range(C_TILES - LAG, C_TILES):
            tensor_mix(k)
            vector_mix(k)
            finish_tensor_columns(k - 1)
            finish_vector_columns(k)
        finish_tensor_columns(C_TILES - 1)
